import numpy as np
import ml_dtypes


def mxq(x, axis, fmt="e4m3"):
    dtype, down = {"e4m3": (ml_dtypes.float8_e4m3fn, 7), "e5m2": (ml_dtypes.float8_e5m2, 14)}[fmt]
    v = np.moveaxis(np.asarray(x, np.float32).astype(ml_dtypes.bfloat16).astype(np.float64), axis, -1)
    blocks = v.reshape(v.shape[:-1] + (-1, 32))
    amax = np.abs(blocks).max(-1, keepdims=True)
    byte = np.maximum(np.where(amax > 0, np.frexp(amax)[1] - 1 + 127, 0) - down, 1)
    scale = np.exp2(byte - 127.0)
    codes = (blocks / scale).astype(np.float32).astype(dtype).astype(np.float64)
    return np.moveaxis((codes * scale).reshape(v.shape), -1, axis)


WIDE = False


def mx_kscale(k):
    if not WIDE:
        return np.ones(k)
    levels = np.array([10, -10, 5, -5, 0])
    if k % 512:
        return np.exp2(np.random.permutation(np.resize(levels, k // 32))).repeat(32)
    a = np.empty((k // 512, 16))
    for p in range(k // 512):
        a[p, :8] = np.random.permutation(np.resize(levels, 8))
        for g in range(8):
            far = levels[np.abs(levels - a[p, g]) >= 10]
            a[p, g + 8] = far[np.random.randint(len(far))]
    return np.exp2(a.ravel()).repeat(32)


BF16 = ml_dtypes.bfloat16


def bf(x):
    return np.asarray(x, np.float32).astype(BF16)


def f64(x):
    return np.asarray(x).astype(np.float64)


B, L, S, D, DA, H, MLP = 2, 3, 256, 1024, 1024, 16, 4096
EPS = 1e-5


def layer_norm(u, g, b):
    mu = u.mean(-1, keepdims=True)
    var = ((u - mu) ** 2).mean(-1, keepdims=True)
    return (u - mu) / np.sqrt(var + EPS) * g + b


def grn(st, stq, W, b, g, be):
    w = np.maximum((stq @ mxq(f64(W), 0, "e4m3")).reshape(B, L, S, D) + f64(b), 0.0)
    n = layer_norm(st, f64(g), f64(be))
    return (w + n).sum(1)


def setup_inputs():
    s = mx_kscale(D)
    r = np.random.standard_normal
    return {"layer_outputs": bf(r((B, L, S, D)) * s),
            "grn_q_W": bf(r((D, D)) / np.sqrt(D) / s[:, None]), "grn_q_b": bf(r(D) * 0.2), "grn_q_g": bf(1.0 + 0.1 * r(D)), "grn_q_be": bf(r(D) * 0.1),
            "grn_k_W": bf(r((D, D)) / np.sqrt(D) / s[:, None]), "grn_k_b": bf(r(D) * 0.2), "grn_k_g": bf(1.0 + 0.1 * r(D)), "grn_k_be": bf(r(D) * 0.1),
            "grn_v_W": bf(r((D, D)) / np.sqrt(D) / s[:, None]), "grn_v_b": bf(r(D) * 0.2), "grn_v_g": bf(1.0 + 0.1 * r(D)), "grn_v_be": bf(r(D) * 0.1)}


def reference(layer_outputs, grn_q_W, grn_q_b, grn_q_g, grn_q_be, grn_k_W, grn_k_b, grn_k_g, grn_k_be, grn_v_W, grn_v_b, grn_v_g, grn_v_be):
    st = f64(layer_outputs)
    stq = mxq(st.reshape(B * L * S, D), 1, "e4m3")
    q = grn(st, stq, grn_q_W, grn_q_b, grn_q_g, grn_q_be)
    k = grn(st, stq, grn_k_W, grn_k_b, grn_k_g, grn_k_be)
    v = grn(st, stq, grn_v_W, grn_v_b, grn_v_g, grn_v_be)
    return q, k, v

@@ -1,0 +1,306 @@
+from contextlib import ExitStack
+
+import concourse.mybir as mybir
+from concourse.masks import make_identity
+
+F32 = mybir.dt.float32
+BF16 = mybir.dt.bfloat16
+U32 = mybir.dt.uint32
+U8 = mybir.dt.uint8
+FP8X4 = mybir.dt.float8_e4m3fn_x4
+ACT = mybir.ActivationFunctionType
+ALU = mybir.AluOpType
+
+P = 128
+PACK = 4
+K_PASS = P * PACK
+
+BATCH, LAYERS, SEQ, DIM = 2, 3, 256, 1024
+EPS = 1e-5
+PROJ = 3
+K_PASSES = DIM // K_PASS
+TOK = BATCH * SEQ
+TOK_TILES = TOK // P
+F_TILES = DIM // P
+GROUP = 4
+GROUP_F = GROUP * P
+GROUPS = PROJ * F_TILES // GROUP
+BANK = 512
+STATS = 6
+STATS_MAX = 512
+
+FLOPS = 2 * BATCH * LAYERS * SEQ * DIM * PROJ * DIM
+
+
+def tile_dcadecoderblock_pa_kernel(
+    tc,
+    layer_outputs,
+    grn_q_W, grn_q_b, grn_q_g, grn_q_be,
+    grn_k_W, grn_k_b, grn_k_g, grn_k_be,
+    grn_v_W, grn_v_b, grn_v_g, grn_v_be,
+    out_0, out_1, out_2,
+):
+    nc = tc.nc
+    weights = [grn_q_W, grn_k_W, grn_v_W]
+    outs = [out_0, out_1, out_2]
+    vectors = [grn_q_b, grn_k_b, grn_v_b, grn_q_g, grn_k_g, grn_v_g, grn_q_be, grn_k_be, grn_v_be]
+    n_ft = PROJ * F_TILES
+
+    with ExitStack() as ctx:
+        const = ctx.enter_context(tc.tile_pool(name="const", bufs=1))
+        x_stage = ctx.enter_context(tc.tile_pool(name="x_stage", bufs=2))
+        w_load = ctx.enter_context(tc.tile_pool(name="w_load", bufs=3))
+        w_stage = ctx.enter_context(tc.tile_pool(name="w_stage", bufs=2))
+        w_keep = ctx.enter_context(tc.tile_pool(name="w_keep", bufs=3))
+        norm_pool = ctx.enter_context(tc.tile_pool(name="norm", bufs=36))
+        sums = ctx.enter_context(tc.tile_pool(name="sums", bufs=14))
+        rows_pool = ctx.enter_context(tc.tile_pool(name="rows", bufs=4))
+        psum_acc = ctx.enter_context(tc.psum_pool(name="psum_acc", bufs=5))
+        psum_tp = ctx.enter_context(tc.psum_pool(name="psum_tp", bufs=3))
+
+        ident_f32 = const.tile([P, P], F32)
+        make_identity(nc, ident_f32[:])
+        ident_bf16 = const.tile([P, P], BF16)
+        make_identity(nc, ident_bf16[:])
+        eps = const.tile([P, 1], F32)
+        nc.vector.memset(eps[:], EPS)
+        table_warm = const.tile([P, 1], F32)
+        nc.scalar.activation(out=table_warm[:], in_=eps[:], func=ACT.Sqrt)
+
+        x_sb = const.tile([P, LAYERS * TOK_TILES, DIM], BF16)
+
+        def load_layer(l):
+            for b in range(BATCH):
+                rt = l * TOK_TILES + 2 * b
+                nc.sync.dma_start(
+                    out=x_sb[:, rt : rt + 2, :],
+                    in_=layer_outputs[b, l, :, :].rearrange("(h p) d -> p h d", p=P),
+                )
+
+        w_raw = {}
+
+        def load_weights(n):
+            t, half = divmod(n, 2)
+            w_raw[n] = w_load.tile([P, K_PASSES, PACK, GROUP_F], BF16, name="w_raw")
+            for g in range(K_PASSES):
+                nc.sync.dma_start(
+                    out=w_raw[n][:, g, :, :],
+                    in_=weights[t][g * K_PASS : (g + 1) * K_PASS, half * GROUP_F : (half + 1) * GROUP_F].rearrange(
+                        "(p j) c -> p j c", j=PACK
+                    ),
+                )
+
+        vec_rows = const.tile([P, P], BF16)
+        nc.vector.memset(vec_rows[:], 0.0)
+        for v, vec in enumerate(vectors):
+            nc.scalar.dma_start(
+                out=vec_rows[v * F_TILES : (v + 1) * F_TILES, :],
+                in_=vec.rearrange("(r c) -> r c", c=P),
+            )
+
+        load_layer(0)
+        load_weights(0)
+        load_layer(1)
+        load_layer(2)
+        load_weights(1)
+        load_weights(2)
+
+        x_codes = const.tile([P, LAYERS * K_PASSES * TOK], U32, align_bytes=64)
+        x_scales = const.tile([P, LAYERS * K_PASSES * TOK], U8, align_bytes=64)
+
+        def quantise_layer(l):
+            grouped = x_stage.tile([P, K_PASSES * TOK * PACK], BF16, align_bytes=64)
+            grouped_words = grouped[:].bitcast(F32).rearrange("p (g r u) -> p g r u", g=K_PASSES, u=2)
+            for j in range(TOK_TILES):
+                x_words = x_sb[:, l * TOK_TILES + j, :].bitcast(F32)
+                xt = psum_tp.tile([P, BANK], F32, tag="tp")
+                for gu in range(BANK // P):
+                    g, u = divmod(gu, 2)
+                    nc.tensor.transpose(
+                        xt[:, gu * P : (gu + 1) * P], x_words[:, 2 * P * g + u : 2 * P * (g + 1) : 2], ident_f32[:]
+                    )
+                nc.scalar.copy(
+                    out=grouped_words[:, :, j * P : (j + 1) * P, :],
+                    in_=xt[:].rearrange("p (g u r) -> p g r u", g=K_PASSES, u=2),
+                )
+            cols = slice(l * K_PASSES * TOK, (l + 1) * K_PASSES * TOK)
+            nc.vector.quantize_mx(out=x_codes[:, cols].bitcast(FP8X4), scales=x_scales[:, cols], in_=grouped[:])
+
+        w_grouped = {}
+        w_codes = {}
+        w_scales = {}
+
+        def regroup_weights(n):
+            w_grouped[n] = w_stage.tile([P, K_PASSES, GROUP_F, PACK], BF16, align_bytes=64, name="w_grouped")
+            for g in range(K_PASSES):
+                dst = w_grouped[n][:, g, :, :].rearrange("p (c i) t -> p c t i", i=4)
+                src = w_raw[n][:, g, :, :].rearrange("p t (c i) -> p c t i", i=4)
+                if g == 0:
+                    nc.vector.tensor_copy(out=dst, in_=src)
+                else:
+                    nc.scalar.copy(out=dst, in_=src)
+
+        def quantise_weights(n):
+            w_codes[n] = w_keep.tile([P, K_PASSES * GROUP_F], U32, align_bytes=64, name="w_codes")
+            w_scales[n] = w_keep.tile([P, K_PASSES * GROUP_F], U8, align_bytes=64, name="w_scales")
+            nc.vector.quantize_mx(
+                out=w_codes[n][:].bitcast(FP8X4),
+                scales=w_scales[n][:],
+                in_=w_grouped[n][:].rearrange("p g c t -> p (g c t)"),
+            )
+
+        params = const.tile([P, P], F32)
+        neg_bias = const.tile([P, n_ft], F32)
+        shift3 = const.tile([P, n_ft], F32)
+        const_term = const.tile([P, n_ft], F32)
+
+        def spread_vectors():
+            vec_cols = psum_tp.tile([P, P], BF16, tag="tp")
+            nc.tensor.transpose(vec_cols[:], vec_rows[:], ident_bf16[:])
+            nc.vector.tensor_copy(out=params[:], in_=vec_cols[:])
+            bias = params[:, 0:n_ft]
+            shift = params[:, 2 * n_ft : 3 * n_ft]
+            nc.vector.tensor_scalar_mul(out=neg_bias[:], in0=bias, scalar1=-1.0)
+            nc.vector.tensor_scalar_mul(out=shift3[:], in0=shift, scalar1=float(LAYERS))
+            nc.vector.scalar_tensor_tensor(
+                out=const_term[:], in0=bias, scalar=float(LAYERS - 1), in1=shift3[:], op0=ALU.mult, op1=ALU.add
+            )
+
+        relu_sum = {}
+
+        def project(n, l):
+            for i in range(GROUP):
+                ft = n * GROUP + i
+                acc = psum_acc.tile([P, TOK], F32, tag="acc")
+                for g in range(K_PASSES):
+                    w_cols = slice(g * GROUP_F + i * P, g * GROUP_F + (i + 1) * P)
+                    x_cols = slice((l * K_PASSES + g) * TOK, (l * K_PASSES + g + 1) * TOK)
+                    nc.tensor.matmul_mx(
+                        out=acc[:],
+                        lhsT=w_codes[n][:, w_cols].bitcast(FP8X4),
+                        lhsT_scale=w_scales[n][:, w_cols],
+                        rhs=x_codes[:, x_cols].bitcast(FP8X4),
+                        rhs_scale=x_scales[:, x_cols],
+                        start=(g == 0),
+                        stop=(g == K_PASSES - 1),
+                    )
+                if l == 0:
+                    relu_sum[ft] = sums.tile([P, TOK], F32, name="relu_sum")
+                    nc.scalar.activation(
+                        out=relu_sum[ft][:], in_=acc[:], func=ACT.Relu, bias=params[:, ft : ft + 1], scale=1.0
+                    )
+                else:
+                    nc.vector.scalar_tensor_tensor(
+                        out=relu_sum[ft][:],
+                        in0=acc[:],
+                        scalar=neg_bias[:, ft : ft + 1],
+                        in1=relu_sum[ft][:],
+                        op0=ALU.max,
+                        op1=ALU.add,
+                    )
+
+        n_rt = LAYERS * TOK_TILES
+        chunks = DIM // STATS_MAX
+        stats = const.tile([P, n_rt, chunks, STATS], F32)
+        mean_var = const.tile([P, n_rt, 2], F32)
+        std = const.tile([P, n_rt], F32)
+        rstd = const.tile([P, n_rt], F32)
+        neg_mean = const.tile([P, n_rt], F32)
+        z_part = {}
+        ln_term = {}
+
+        def layer_statistics(l):
+            for j in range(TOK_TILES):
+                rt = l * TOK_TILES + j
+                for c in range(chunks):
+                    nc.vector.bn_stats(out=stats[:, rt, c, :], in_=x_sb[:, rt, c * STATS_MAX : (c + 1) * STATS_MAX])
+                nc.vector.bn_aggr(out=mean_var[:, rt, :], in_=stats[:, rt, :, :].rearrange("p c s -> p (c s)"))
+            rts = slice(l * TOK_TILES, (l + 1) * TOK_TILES)
+            nc.scalar.activation(out=std[:, rts], in_=mean_var[:, rts, 1], func=ACT.Sqrt, bias=eps[:, 0:1], scale=1.0)
+            nc.vector.tensor_scalar_mul(out=neg_mean[:, rts], in0=mean_var[:, rts, 0], scalar1=-1.0)
+            nc.vector.reciprocal(out=rstd[:, rts], in_=std[:, rts])
+
+        def normalised_parts(l):
+            for half in range(DIM // BANK):
+                for j in range(TOK_TILES):
+                    rt = l * TOK_TILES + j
+                    z_part[l, j, half] = norm_pool.tile([P, BANK], F32, name="z_part", tag="norm")
+                    nc.gpsimd.tensor_scalar(
+                        out=z_part[l, j, half][:],
+                        in0=x_sb[:, rt, half * BANK : (half + 1) * BANK],
+                        scalar1=neg_mean[:, rt : rt + 1],
+                        scalar2=rstd[:, rt : rt + 1],
+                        op0=ALU.add,
+                        op1=ALU.mult,
+                    )
+
+        def norm_terms(f):
+            half, f_in_half = divmod(f, BANK // P)
+            f_cols = slice(f_in_half * P, (f_in_half + 1) * P)
+            zt = psum_tp.tile([P, BANK], F32, tag="tp")
+            for j in range(TOK_TILES):
+                for l in range(LAYERS):
+                    nc.tensor.matmul(
+                        out=zt[:, j * P : (j + 1) * P],
+                        lhsT=z_part[l, j, half][:, f_cols],
+                        rhs=ident_f32[:],
+                        is_transpose=True,
+                        start=(l == 0),
+                        stop=(l == LAYERS - 1),
+                    )
+            for t in range(PROJ):
+                ft = t * F_TILES + f
+                ln_term[ft] = norm_pool.tile([P, TOK], F32, name="ln_term", tag="norm")
+                nc.scalar.activation(
+                    out=ln_term[ft][:], in_=zt[:], func=ACT.Identity,
+                    scale=params[:, n_ft + ft : n_ft + ft + 1], bias=const_term[:, ft : ft + 1],
+                )
+
+        def finish_group(n):
+            t, half = divmod(n, 2)
+            adder = nc.vector if n == GROUPS - 1 else nc.gpsimd
+            for i in range(GROUP):
+                ft = n * GROUP + i
+                adder.tensor_tensor(out=ln_term[ft][:], in0=ln_term[ft][:], in1=relu_sum[ft][:], op=ALU.add)
+            for j in range(TOK_TILES):
+                b, h = divmod(j, 2)
+                back = psum_tp.tile([P, BANK], F32, tag="tp")
+                for i in range(GROUP):
+                    nc.tensor.transpose(
+                        back[:, i * P : (i + 1) * P], ln_term[n * GROUP + i][:, j * P : (j + 1) * P], ident_f32[:]
+                    )
+                rows = rows_pool.tile([P, GROUP_F], F32)
+                nc.any.tensor_copy(out=rows[:], in_=back[:])
+                nc.sync.dma_start(
+                    out=outs[t][b, h * P : (h + 1) * P, half * GROUP_F : (half + 1) * GROUP_F], in_=rows[:]
+                )
+
+        quantise_layer(0)
+        regroup_weights(0)
+        quantise_weights(0)
+        spread_vectors()
+        quantise_layer(1)
+        project(0, 0)
+        layer_statistics(0)
+        normalised_parts(0)
+        quantise_layer(2)
+        project(0, 1)
+        layer_statistics(1)
+        normalised_parts(1)
+        regroup_weights(1)
+        quantise_weights(1)
+        project(0, 2)
+        layer_statistics(2)
+        normalised_parts(2)
+        for f in range(F_TILES):
+            norm_terms(f)
+        for n in range(1, GROUPS):
+            if n + 2 < GROUPS:
+                load_weights(n + 2)
+            if n + 1 < GROUPS:
+                regroup_weights(n + 1)
+                quantise_weights(n + 1)
+            for l in range(LAYERS):
+                project(n, l)
+            finish_group(n - 1)
+        finish_group(GROUPS - 1)

@@ -24,7 +24,10 @@ TOK_TILES = TOK // P
 F_TILES = DIM // P
 GROUP = 4
 GROUP_F = GROUP * P
+PAIR_F = 2 * P
 GROUPS = PROJ * F_TILES // GROUP
+GROUP_OF = [(n % PROJ, n // PROJ) for n in range(GROUPS)]
+BY_SCALAR = [2, 2, 2, 0, 0, 0]
 BANK = 512
 STATS = 6
 STATS_MAX = 512
@@ -43,7 +46,9 @@ def tile_dcadecoderblock_pa_kernel(
     nc = tc.nc
     weights = [grn_q_W, grn_k_W, grn_v_W]
     outs = [out_0, out_1, out_2]
-    vectors = [grn_q_b, grn_k_b, grn_v_b, grn_q_g, grn_k_g, grn_v_g, grn_q_be, grn_k_be, grn_v_be]
+    biases = [grn_q_b, grn_k_b, grn_v_b]
+    gains = [grn_q_g, grn_k_g, grn_v_g]
+    shifts = [grn_q_be, grn_k_be, grn_v_be]
     n_ft = PROJ * F_TILES
 
     with ExitStack() as ctx:
@@ -52,11 +57,12 @@ def tile_dcadecoderblock_pa_kernel(
         w_load = ctx.enter_context(tc.tile_pool(name="w_load", bufs=3))
         w_stage = ctx.enter_context(tc.tile_pool(name="w_stage", bufs=2))
         w_keep = ctx.enter_context(tc.tile_pool(name="w_keep", bufs=3))
-        norm_pool = ctx.enter_context(tc.tile_pool(name="norm", bufs=36))
-        sums = ctx.enter_context(tc.tile_pool(name="sums", bufs=14))
-        rows_pool = ctx.enter_context(tc.tile_pool(name="rows", bufs=4))
+        norm_pool = ctx.enter_context(tc.tile_pool(name="norm", bufs=32))
+        sums = ctx.enter_context(tc.tile_pool(name="sums", bufs=16))
+        rows_pool = ctx.enter_context(tc.tile_pool(name="rows", bufs=8))
         psum_acc = ctx.enter_context(tc.psum_pool(name="psum_acc", bufs=5))
         psum_tp = ctx.enter_context(tc.psum_pool(name="psum_tp", bufs=3))
+        ctx.enter_context(tc.manual_schedule())
 
         ident_f32 = const.tile([P, P], F32)
         make_identity(nc, ident_f32[:])
@@ -66,6 +72,10 @@ def tile_dcadecoderblock_pa_kernel(
         nc.vector.memset(eps[:], EPS)
         table_warm = const.tile([P, 1], F32)
         nc.scalar.activation(out=table_warm[:], in_=eps[:], func=ACT.Sqrt)
+        bias_rows = const.tile([P, P], BF16)
+        norm_rows = const.tile([P, P], BF16)
+        nc.vector.memset(bias_rows[:], 0.0)
+        nc.vector.memset(norm_rows[:], 0.0)
 
         x_sb = const.tile([P, LAYERS * TOK_TILES, DIM], BF16)
 
@@ -80,7 +90,7 @@ def tile_dcadecoderblock_pa_kernel(
         w_raw = {}
 
         def load_weights(n):
-            t, half = divmod(n, 2)
+            t, half = GROUP_OF[n]
             w_raw[n] = w_load.tile([P, K_PASSES, PACK, GROUP_F], BF16, name="w_raw")
             for g in range(K_PASSES):
                 nc.sync.dma_start(
@@ -90,114 +100,134 @@ def tile_dcadecoderblock_pa_kernel(
                     ),
                 )
 
-        vec_rows = const.tile([P, P], BF16)
-        nc.vector.memset(vec_rows[:], 0.0)
-        for v, vec in enumerate(vectors):
-            nc.scalar.dma_start(
-                out=vec_rows[v * F_TILES : (v + 1) * F_TILES, :],
-                in_=vec.rearrange("(r c) -> r c", c=P),
-            )
+        def load_vectors(rows, vecs):
+            for v, vec in enumerate(vecs):
+                nc.sync.dma_start(
+                    out=rows[v * F_TILES : (v + 1) * F_TILES, :], in_=vec.rearrange("(r c) -> r c", c=P)
+                )
 
         load_layer(0)
         load_weights(0)
+        load_vectors(bias_rows, biases)
         load_layer(1)
         load_layer(2)
         load_weights(1)
+        load_vectors(norm_rows, gains + shifts)
         load_weights(2)
 
         x_codes = const.tile([P, LAYERS * K_PASSES * TOK], U32, align_bytes=64)
         x_scales = const.tile([P, LAYERS * K_PASSES * TOK], U8, align_bytes=64)
+        grouped = {}
+
+        def turn_tokens(l, j):
+            if j == 0:
+                grouped[l] = x_stage.tile([P, K_PASSES * TOK * PACK], BF16, align_bytes=64, name="grouped")
+            grouped_words = grouped[l][:].bitcast(F32).rearrange("p (g r u) -> p g r u", g=K_PASSES, u=2)
+            x_words = x_sb[:, l * TOK_TILES + j, :].bitcast(F32)
+            xt = psum_tp.tile([P, BANK], F32, tag="tp", name="xt")
+            for gu in range(BANK // P):
+                g, u = divmod(gu, 2)
+                nc.tensor.transpose(
+                    xt[:, gu * P : (gu + 1) * P], x_words[:, 2 * P * g + u : 2 * P * (g + 1) : 2], ident_f32[:]
+                )
+            nc.scalar.copy(
+                out=grouped_words[:, :, j * P : (j + 1) * P, :],
+                in_=xt[:].rearrange("p (g u r) -> p g r u", g=K_PASSES, u=2),
+            )
 
         def quantise_layer(l):
-            grouped = x_stage.tile([P, K_PASSES * TOK * PACK], BF16, align_bytes=64)
-            grouped_words = grouped[:].bitcast(F32).rearrange("p (g r u) -> p g r u", g=K_PASSES, u=2)
-            for j in range(TOK_TILES):
-                x_words = x_sb[:, l * TOK_TILES + j, :].bitcast(F32)
-                xt = psum_tp.tile([P, BANK], F32, tag="tp")
-                for gu in range(BANK // P):
-                    g, u = divmod(gu, 2)
-                    nc.tensor.transpose(
-                        xt[:, gu * P : (gu + 1) * P], x_words[:, 2 * P * g + u : 2 * P * (g + 1) : 2], ident_f32[:]
-                    )
-                nc.scalar.copy(
-                    out=grouped_words[:, :, j * P : (j + 1) * P, :],
-                    in_=xt[:].rearrange("p (g u r) -> p g r u", g=K_PASSES, u=2),
-                )
             cols = slice(l * K_PASSES * TOK, (l + 1) * K_PASSES * TOK)
-            nc.vector.quantize_mx(out=x_codes[:, cols].bitcast(FP8X4), scales=x_scales[:, cols], in_=grouped[:])
+            nc.vector.quantize_mx(out=x_codes[:, cols].bitcast(FP8X4), scales=x_scales[:, cols], in_=grouped[l][:])
 
         w_grouped = {}
         w_codes = {}
         w_scales = {}
 
-        def regroup_weights(n):
-            w_grouped[n] = w_stage.tile([P, K_PASSES, GROUP_F, PACK], BF16, align_bytes=64, name="w_grouped")
-            for g in range(K_PASSES):
-                dst = w_grouped[n][:, g, :, :].rearrange("p (c i) t -> p c t i", i=4)
-                src = w_raw[n][:, g, :, :].rearrange("p t (c i) -> p c t i", i=4)
-                if g == 0:
-                    nc.vector.tensor_copy(out=dst, in_=src)
-                else:
-                    nc.scalar.copy(out=dst, in_=src)
+        def regroup_weights(n, g, engine):
+            if n not in w_grouped:
+                w_grouped[n] = w_stage.tile([P, K_PASSES, GROUP_F, PACK], BF16, align_bytes=64, name="w_grouped")
+            dst = w_grouped[n][:, g, :, :].rearrange("p (c i) t -> p c t i", i=4)
+            src = w_raw[n][:, g, :, :].rearrange("p t (c i) -> p c t i", i=4)
+            if engine == "vector":
+                nc.vector.tensor_copy(out=dst, in_=src)
+            elif engine == "scalar":
+                nc.scalar.copy(out=dst, in_=src)
+            else:
+                dst = w_grouped[n][:, g, :, :]
+                src = w_raw[n][:, g, :, :].rearrange("p t c -> p c t")
+                nc.gpsimd.tensor_scalar(out=dst, in0=src, scalar1=1.0, scalar2=0.0, op0=ALU.mult, op1=ALU.add)
 
-        def quantise_weights(n):
-            w_codes[n] = w_keep.tile([P, K_PASSES * GROUP_F], U32, align_bytes=64, name="w_codes")
-            w_scales[n] = w_keep.tile([P, K_PASSES * GROUP_F], U8, align_bytes=64, name="w_scales")
+        def quantise_weights(n, g_from, g_to):
+            if g_from == 0:
+                w_codes[n] = w_keep.tile([P, K_PASSES * GROUP_F], U32, align_bytes=64, name="w_codes")
+                w_scales[n] = w_keep.tile([P, K_PASSES * GROUP_F], U8, align_bytes=64, name="w_scales")
+            cols = slice(g_from * GROUP_F, g_to * GROUP_F)
             nc.vector.quantize_mx(
-                out=w_codes[n][:].bitcast(FP8X4),
-                scales=w_scales[n][:],
-                in_=w_grouped[n][:].rearrange("p g c t -> p (g c t)"),
+                out=w_codes[n][:, cols].bitcast(FP8X4),
+                scales=w_scales[n][:, cols],
+                in_=w_grouped[n][:, g_from:g_to, :, :].rearrange("p g c t -> p (g c t)"),
             )
 
-        params = const.tile([P, P], F32)
+        bias = const.tile([P, P], F32)
+        norm_params = const.tile([P, P], F32)
         neg_bias = const.tile([P, n_ft], F32)
         shift3 = const.tile([P, n_ft], F32)
-        const_term = const.tile([P, n_ft], F32)
+        owed = {m: const.tile([P, n_ft], F32, name="owed%d" % m) for m in set(BY_SCALAR)}
 
-        def spread_vectors():
-            vec_cols = psum_tp.tile([P, P], BF16, tag="tp")
-            nc.tensor.transpose(vec_cols[:], vec_rows[:], ident_bf16[:])
-            nc.vector.tensor_copy(out=params[:], in_=vec_cols[:])
-            bias = params[:, 0:n_ft]
-            shift = params[:, 2 * n_ft : 3 * n_ft]
-            nc.vector.tensor_scalar_mul(out=neg_bias[:], in0=bias, scalar1=-1.0)
-            nc.vector.tensor_scalar_mul(out=shift3[:], in0=shift, scalar1=float(LAYERS))
-            nc.vector.scalar_tensor_tensor(
-                out=const_term[:], in0=bias, scalar=float(LAYERS - 1), in1=shift3[:], op0=ALU.mult, op1=ALU.add
+        def spread_rows(rows, table):
+            cols = psum_tp.tile([P, P], BF16, tag="tp", name="cols")
+            nc.tensor.transpose(cols[:], rows[:], ident_bf16[:])
+            nc.scalar.copy(out=table[:], in_=cols[:])
+
+        def spread_biases():
+            spread_rows(bias_rows, bias)
+            nc.vector.tensor_scalar_mul(out=neg_bias[:], in0=bias[:, 0:n_ft], scalar1=-1.0)
+
+        def spread_norm_params():
+            spread_rows(norm_rows, norm_params)
+            nc.vector.tensor_scalar_mul(
+                out=shift3[:], in0=norm_params[:, n_ft : 2 * n_ft], scalar1=float(LAYERS)
             )
 
-        relu_sum = {}
+        def owed_terms():
+            for m in set(BY_SCALAR):
+                nc.vector.scalar_tensor_tensor(
+                    out=owed[m][:], in0=bias[:, 0:n_ft], scalar=float(LAYERS - m), in1=shift3[:], op0=ALU.mult, op1=ALU.add
+                )
 
-        def project(n, l):
-            for i in range(GROUP):
-                ft = n * GROUP + i
-                acc = psum_acc.tile([P, TOK], F32, tag="acc")
-                for g in range(K_PASSES):
-                    w_cols = slice(g * GROUP_F + i * P, g * GROUP_F + (i + 1) * P)
-                    x_cols = slice((l * K_PASSES + g) * TOK, (l * K_PASSES + g + 1) * TOK)
-                    nc.tensor.matmul_mx(
-                        out=acc[:],
-                        lhsT=w_codes[n][:, w_cols].bitcast(FP8X4),
-                        lhsT_scale=w_scales[n][:, w_cols],
-                        rhs=x_codes[:, x_cols].bitcast(FP8X4),
-                        rhs_scale=x_scales[:, x_cols],
-                        start=(g == 0),
-                        stop=(g == K_PASSES - 1),
-                    )
-                if l == 0:
-                    relu_sum[ft] = sums.tile([P, TOK], F32, name="relu_sum")
-                    nc.scalar.activation(
-                        out=relu_sum[ft][:], in_=acc[:], func=ACT.Relu, bias=params[:, ft : ft + 1], scale=1.0
-                    )
-                else:
-                    nc.vector.scalar_tensor_tensor(
-                        out=relu_sum[ft][:],
-                        in0=acc[:],
-                        scalar=neg_bias[:, ft : ft + 1],
-                        in1=relu_sum[ft][:],
-                        op0=ALU.max,
-                        op1=ALU.add,
-                    )
+        relus = {}
+        ln_term = {}
+
+        def feature_tile(n, i):
+            t, half = GROUP_OF[n]
+            return t * F_TILES + half * GROUP + i
+
+        def project(n, i, l):
+            ft = feature_tile(n, i)
+            acc = psum_acc.tile([P, TOK], F32, tag="acc", name="acc")
+            for g in range(K_PASSES):
+                w_cols = slice(g * GROUP_F + i * P, g * GROUP_F + (i + 1) * P)
+                x_cols = slice((l * K_PASSES + g) * TOK, (l * K_PASSES + g + 1) * TOK)
+                nc.tensor.matmul_mx(
+                    out=acc[:],
+                    lhsT=w_codes[n][:, w_cols].bitcast(FP8X4),
+                    lhsT_scale=w_scales[n][:, w_cols],
+                    rhs=x_codes[:, x_cols].bitcast(FP8X4),
+                    rhs_scale=x_scales[:, x_cols],
+                    start=(g == 0),
+                    stop=(g == K_PASSES - 1),
+                )
+            if l < BY_SCALAR[n]:
+                relu = sums.tile([P, TOK], F32, name="relu")
+                nc.scalar.activation(
+                    out=relu[:], in_=acc[:], func=ACT.Relu, bias=bias[:, ft : ft + 1], scale=1.0
+                )
+                relus.setdefault(ft, []).append(relu)
+            else:
+                total = relus[ft][0] if BY_SCALAR[n] else ln_term[ft]
+                nc.vector.scalar_tensor_tensor(
+                    out=total[:], in0=acc[:], scalar=neg_bias[:, ft : ft + 1], in1=total[:], op0=ALU.max, op1=ALU.add
+                )
 
         n_rt = LAYERS * TOK_TILES
         chunks = DIM // STATS_MAX
@@ -207,37 +237,43 @@ def tile_dcadecoderblock_pa_kernel(
         rstd = const.tile([P, n_rt], F32)
         neg_mean = const.tile([P, n_rt], F32)
         z_part = {}
-        ln_term = {}
 
-        def layer_statistics(l):
+        def tile_statistics(l, j):
+            rt = l * TOK_TILES + j
+            for c in range(chunks):
+                nc.vector.bn_stats(out=stats[:, rt, c, :], in_=x_sb[:, rt, c * STATS_MAX : (c + 1) * STATS_MAX])
+
+        def aggregate(l):
             for j in range(TOK_TILES):
                 rt = l * TOK_TILES + j
-                for c in range(chunks):
-                    nc.vector.bn_stats(out=stats[:, rt, c, :], in_=x_sb[:, rt, c * STATS_MAX : (c + 1) * STATS_MAX])
                 nc.vector.bn_aggr(out=mean_var[:, rt, :], in_=stats[:, rt, :, :].rearrange("p c s -> p (c s)"))
+
+        def layer_scales(l):
             rts = slice(l * TOK_TILES, (l + 1) * TOK_TILES)
             nc.scalar.activation(out=std[:, rts], in_=mean_var[:, rts, 1], func=ACT.Sqrt, bias=eps[:, 0:1], scale=1.0)
             nc.vector.tensor_scalar_mul(out=neg_mean[:, rts], in0=mean_var[:, rts, 0], scalar1=-1.0)
+
+        def layer_inverse(l):
+            rts = slice(l * TOK_TILES, (l + 1) * TOK_TILES)
             nc.vector.reciprocal(out=rstd[:, rts], in_=std[:, rts])
 
-        def normalised_parts(l):
-            for half in range(DIM // BANK):
-                for j in range(TOK_TILES):
-                    rt = l * TOK_TILES + j
-                    z_part[l, j, half] = norm_pool.tile([P, BANK], F32, name="z_part", tag="norm")
-                    nc.gpsimd.tensor_scalar(
-                        out=z_part[l, j, half][:],
-                        in0=x_sb[:, rt, half * BANK : (half + 1) * BANK],
-                        scalar1=neg_mean[:, rt : rt + 1],
-                        scalar2=rstd[:, rt : rt + 1],
-                        op0=ALU.add,
-                        op1=ALU.mult,
-                    )
+        def normalised_parts(l, half):
+            for j in range(TOK_TILES):
+                rt = l * TOK_TILES + j
+                z_part[l, j, half] = norm_pool.tile([P, BANK], F32, name="z_part", tag="norm")
+                nc.gpsimd.tensor_scalar(
+                    out=z_part[l, j, half][:],
+                    in0=x_sb[:, rt, half * BANK : (half + 1) * BANK],
+                    scalar1=neg_mean[:, rt : rt + 1],
+                    scalar2=rstd[:, rt : rt + 1],
+                    op0=ALU.add,
+                    op1=ALU.mult,
+                )
 
-        def norm_terms(f):
+        def norm_terms(f, ts=range(PROJ)):
             half, f_in_half = divmod(f, BANK // P)
             f_cols = slice(f_in_half * P, (f_in_half + 1) * P)
-            zt = psum_tp.tile([P, BANK], F32, tag="tp")
+            zt = psum_tp.tile([P, BANK], F32, tag="tp", name="zt")
             for j in range(TOK_TILES):
                 for l in range(LAYERS):
                     nc.tensor.matmul(
@@ -248,59 +284,152 @@ def tile_dcadecoderblock_pa_kernel(
                         start=(l == 0),
                         stop=(l == LAYERS - 1),
                     )
-            for t in range(PROJ):
+            for t in ts:
                 ft = t * F_TILES + f
+                n = half * PROJ + t
                 ln_term[ft] = norm_pool.tile([P, TOK], F32, name="ln_term", tag="norm")
                 nc.scalar.activation(
                     out=ln_term[ft][:], in_=zt[:], func=ACT.Identity,
-                    scale=params[:, n_ft + ft : n_ft + ft + 1], bias=const_term[:, ft : ft + 1],
+                    scale=norm_params[:, ft : ft + 1], bias=owed[BY_SCALAR[n]][:, ft : ft + 1],
                 )
 
-        def finish_group(n):
-            t, half = divmod(n, 2)
-            adder = nc.vector if n == GROUPS - 1 else nc.gpsimd
-            for i in range(GROUP):
-                ft = n * GROUP + i
-                adder.tensor_tensor(out=ln_term[ft][:], in0=ln_term[ft][:], in1=relu_sum[ft][:], op=ALU.add)
-            for j in range(TOK_TILES):
-                b, h = divmod(j, 2)
-                back = psum_tp.tile([P, BANK], F32, tag="tp")
-                for i in range(GROUP):
+        def merge_layers(n, i):
+            ft = feature_tile(n, i)
+            first = relus[ft][0]
+            for other in relus[ft][1:]:
+                nc.gpsimd.tensor_tensor(out=first[:], in0=first[:], in1=other[:], op=ALU.add)
+
+        def merge(n, i):
+            ft = feature_tile(n, i)
+            nc.gpsimd.tensor_tensor(out=ln_term[ft][:], in0=ln_term[ft][:], in1=relus[ft][0][:], op=ALU.add)
+
+        def turn_back(n, pair, b, engine):
+            t, half = GROUP_OF[n]
+            back = psum_tp.tile([P, SEQ // P, PAIR_F], F32, tag="tp", name="back")
+            for h in range(SEQ // P):
+                j = b * (SEQ // P) + h
+                for e in range(2):
+                    ft = feature_tile(n, 2 * pair + e)
                     nc.tensor.transpose(
-                        back[:, i * P : (i + 1) * P], ln_term[n * GROUP + i][:, j * P : (j + 1) * P], ident_f32[:]
+                        back[:, h, e * P : (e + 1) * P], ln_term[ft][:, j * P : (j + 1) * P], ident_f32[:]
                     )
-                rows = rows_pool.tile([P, GROUP_F], F32)
-                nc.any.tensor_copy(out=rows[:], in_=back[:])
-                nc.sync.dma_start(
-                    out=outs[t][b, h * P : (h + 1) * P, half * GROUP_F : (half + 1) * GROUP_F], in_=rows[:]
-                )
+            rows = rows_pool.tile([P, SEQ // P, PAIR_F], F32, name="rows")
+            if engine == "vector":
+                nc.vector.tensor_copy(out=rows[:], in_=back[:])
+            else:
+                nc.scalar.copy(out=rows[:], in_=back[:])
+            f0 = half * GROUP_F + pair * PAIR_F
+            nc.sync.dma_start(
+                out=outs[t][b, :, f0 : f0 + PAIR_F].rearrange("(h p) f -> p h f", p=P), in_=rows[:]
+            )
 
-        quantise_layer(0)
-        regroup_weights(0)
-        quantise_weights(0)
-        spread_vectors()
-        quantise_layer(1)
-        project(0, 0)
-        layer_statistics(0)
-        normalised_parts(0)
-        quantise_layer(2)
-        project(0, 1)
-        layer_statistics(1)
-        normalised_parts(1)
-        regroup_weights(1)
-        quantise_weights(1)
-        project(0, 2)
-        layer_statistics(2)
-        normalised_parts(2)
-        for f in range(F_TILES):
-            norm_terms(f)
-        for n in range(1, GROUPS):
-            if n + 2 < GROUPS:
-                load_weights(n + 2)
-            if n + 1 < GROUPS:
-                regroup_weights(n + 1)
-                quantise_weights(n + 1)
+        def stat_tiles(l, *js):
+            for j in js:
+                tile_statistics(l, j)
+
+        def turn_layer(l):
+            for j in range(TOK_TILES):
+                turn_tokens(l, j)
+
+        def project_group(n, l):
+            for i in range(GROUP):
+                project(n, i, l)
+
+        def project_pair(n, pair):
             for l in range(LAYERS):
-                project(n, l)
-            finish_group(n - 1)
-        finish_group(GROUPS - 1)
+                for i in (2 * pair, 2 * pair + 1):
+                    project(n, i, l)
+
+        def turn_pair_back(n, pair, *engines):
+            for b in range(BATCH):
+                turn_back(n, pair, b, engines[b])
+
+        turn_layer(0)
+        stat_tiles(0, 0)
+        regroup_weights(0, 0, "vector")
+        regroup_weights(0, 1, "scalar")
+        quantise_layer(0)
+        quantise_weights(0, 0, 1)
+        stat_tiles(0, 1)
+        turn_layer(1)
+        quantise_weights(0, 1, 2)
+        stat_tiles(0, 2)
+        spread_biases()
+        turn_layer(2)
+        quantise_layer(1)
+        project_group(0, 0)
+        stat_tiles(0, 3)
+        quantise_layer(2)
+        aggregate(0)
+        layer_scales(0)
+        regroup_weights(1, 0, "gpsimd")
+        regroup_weights(1, 1, "gpsimd")
+        project_group(0, 1)
+        stat_tiles(1, 0)
+        layer_inverse(0)
+        stat_tiles(1, 1, 2)
+        quantise_weights(1, 0, 2)
+        project_group(0, 2)
+        regroup_weights(2, 0, "gpsimd")
+        load_weights(3)
+        regroup_weights(2, 1, "scalar")
+        stat_tiles(1, 3)
+        stat_tiles(2, 0)
+        aggregate(1)
+        project_pair(1, 0)
+        layer_scales(1)
+        for i in range(GROUP):
+            merge_layers(0, i)
+        quantise_weights(2, 0, 2)
+        layer_inverse(1)
+        stat_tiles(2, 1)
+        normalised_parts(0, 1)
+        normalised_parts(1, 1)
+        project_pair(1, 1)
+        stat_tiles(2, 2, 3)
+        load_weights(4)
+        regroup_weights(3, 0, "scalar")
+        aggregate(2)
+        spread_norm_params()
+        layer_scales(2)
+        project_pair(2, 0)
+        owed_terms()
+        layer_inverse(2)
+        normalised_parts(2, 1)
+        normalised_parts(0, 0)
+        normalised_parts(1, 0)
+        normalised_parts(2, 0)
+        regroup_weights(3, 1, "vector")
+        project_pair(2, 1)
+        quantise_weights(3, 0, 2)
+        load_weights(5)
+        for f in range(4, 7):
+            norm_terms(f)
+        for n in range(1, 3):
+            for i in range(GROUP):
+                merge_layers(n, i)
+        backs = [(n, pair) for n in range(GROUPS) for pair in range(2)]
+        for n in range(3, GROUPS):
+            for pair in range(2):
+                project_pair(n, pair)
+                if n + 1 < GROUPS:
+                    if pair == 0:
+                        regroup_weights(n + 1, 0, "vector")
+                        regroup_weights(n + 1, 1, "vector")
+                    else:
+                        quantise_weights(n + 1, 0, 2)
+                if n == 3:
+                    if pair == 0:
+                        norm_terms(7)
+                        norm_terms(0)
+                    else:
+                        for f in range(1, 4):
+                            norm_terms(f)
+                        for m in range(3):
+                            for i in range(GROUP):
+                                merge(m, i)
+                else:
+                    for m in range(2 if n == 4 else 3):
+                        turn_pair_back(*backs.pop(0), "scalar", "scalar")
+        while backs:
+            turn_pair_back(*backs.pop(0), "scalar", "vector")

@@ -27,7 +27,7 @@ GROUP_F = GROUP * P
 PAIR_F = 2 * P
 GROUPS = PROJ * F_TILES // GROUP
 GROUP_OF = [(n % PROJ, n // PROJ) for n in range(GROUPS)]
-BY_SCALAR = [2, 2, 2, 0, 0, 0]
+BY_SCALAR = [2, 2, 1, 0, 0, 0]
 BANK = 512
 STATS = 6
 STATS_MAX = 512
@@ -58,7 +58,7 @@ def tile_dcadecoderblock_pa_kernel(
         w_stage = ctx.enter_context(tc.tile_pool(name="w_stage", bufs=2))
         w_keep = ctx.enter_context(tc.tile_pool(name="w_keep", bufs=3))
         norm_pool = ctx.enter_context(tc.tile_pool(name="norm", bufs=32))
-        sums = ctx.enter_context(tc.tile_pool(name="sums", bufs=16))
+        sums = ctx.enter_context(tc.tile_pool(name="sums", bufs=20))
         rows_pool = ctx.enter_context(tc.tile_pool(name="rows", bufs=8))
         psum_acc = ctx.enter_context(tc.psum_pool(name="psum_acc", bufs=5))
         psum_tp = ctx.enter_context(tc.psum_pool(name="psum_tp", bufs=3))
@@ -68,10 +68,10 @@ def tile_dcadecoderblock_pa_kernel(
         make_identity(nc, ident_f32[:])
         ident_bf16 = const.tile([P, P], BF16)
         make_identity(nc, ident_bf16[:])
-        eps = const.tile([P, 1], F32)
-        nc.vector.memset(eps[:], EPS)
+        minus_half = const.tile([P, TOK_TILES], F32)
+        nc.vector.memset(minus_half[:], -0.5)
         table_warm = const.tile([P, 1], F32)
-        nc.scalar.activation(out=table_warm[:], in_=eps[:], func=ACT.Sqrt)
+        nc.scalar.activation(out=table_warm[:], in_=minus_half[:, 0:1], func=ACT.Relu)
         bias_rows = const.tile([P, P], BF16)
         norm_rows = const.tile([P, P], BF16)
         nc.vector.memset(bias_rows[:], 0.0)
@@ -107,9 +107,9 @@ def tile_dcadecoderblock_pa_kernel(
                 )
 
         load_layer(0)
+        load_layer(1)
         load_weights(0)
         load_vectors(bias_rows, biases)
-        load_layer(1)
         load_layer(2)
         load_weights(1)
         load_vectors(norm_rows, gains + shifts)
@@ -233,9 +233,8 @@ def tile_dcadecoderblock_pa_kernel(
         chunks = DIM // STATS_MAX
         stats = const.tile([P, n_rt, chunks, STATS], F32)
         mean_var = const.tile([P, n_rt, 2], F32)
-        std = const.tile([P, n_rt], F32)
+        var_eps = const.tile([P, n_rt], F32)
         rstd = const.tile([P, n_rt], F32)
-        neg_mean = const.tile([P, n_rt], F32)
         z_part = {}
 
         def tile_statistics(l, j):
@@ -250,23 +249,21 @@ def tile_dcadecoderblock_pa_kernel(
 
         def layer_scales(l):
             rts = slice(l * TOK_TILES, (l + 1) * TOK_TILES)
-            nc.scalar.activation(out=std[:, rts], in_=mean_var[:, rts, 1], func=ACT.Sqrt, bias=eps[:, 0:1], scale=1.0)
-            nc.vector.tensor_scalar_mul(out=neg_mean[:, rts], in0=mean_var[:, rts, 0], scalar1=-1.0)
+            nc.gpsimd.tensor_scalar(
+                out=var_eps[:, rts], in0=mean_var[:, rts, 1], scalar1=EPS, scalar2=0.0, op0=ALU.add, op1=ALU.add
+            )
+            nc.gpsimd.tensor_tensor(out=rstd[:, rts], in0=var_eps[:, rts], in1=minus_half[:], op=ALU.pow)
 
-        def layer_inverse(l):
-            rts = slice(l * TOK_TILES, (l + 1) * TOK_TILES)
-            nc.vector.reciprocal(out=rstd[:, rts], in_=std[:, rts])
-
-        def normalised_parts(l, half):
+        def normalised_parts(l, half, engine):
             for j in range(TOK_TILES):
                 rt = l * TOK_TILES + j
                 z_part[l, j, half] = norm_pool.tile([P, BANK], F32, name="z_part", tag="norm")
-                nc.gpsimd.tensor_scalar(
+                engine.tensor_scalar(
                     out=z_part[l, j, half][:],
                     in0=x_sb[:, rt, half * BANK : (half + 1) * BANK],
-                    scalar1=neg_mean[:, rt : rt + 1],
+                    scalar1=mean_var[:, rt, 0:1],
                     scalar2=rstd[:, rt : rt + 1],
-                    op0=ALU.add,
+                    op0=ALU.subtract,
                     op1=ALU.mult,
                 )
 
@@ -345,69 +342,64 @@ def tile_dcadecoderblock_pa_kernel(
                 turn_back(n, pair, b, engines[b])
 
         turn_layer(0)
-        stat_tiles(0, 0)
-        regroup_weights(0, 0, "vector")
-        regroup_weights(0, 1, "scalar")
-        quantise_layer(0)
-        quantise_weights(0, 0, 1)
-        stat_tiles(0, 1)
+        stat_tiles(0, 0, 1)
         turn_layer(1)
+        quantise_layer(0)
+        regroup_weights(0, 1, "scalar")
+        regroup_weights(0, 0, "vector")
+        quantise_weights(0, 0, 1)
+        quantise_layer(1)
         quantise_weights(0, 1, 2)
         stat_tiles(0, 2)
         spread_biases()
         turn_layer(2)
-        quantise_layer(1)
-        project_group(0, 0)
         stat_tiles(0, 3)
-        quantise_layer(2)
+        project_group(0, 0)
         aggregate(0)
-        layer_scales(0)
+        quantise_layer(2)
         regroup_weights(1, 0, "gpsimd")
-        regroup_weights(1, 1, "gpsimd")
+        regroup_weights(1, 1, "vector")
+        layer_scales(0)
         project_group(0, 1)
         stat_tiles(1, 0)
-        layer_inverse(0)
-        stat_tiles(1, 1, 2)
         quantise_weights(1, 0, 2)
+        stat_tiles(1, 1, 2)
         project_group(0, 2)
-        regroup_weights(2, 0, "gpsimd")
+        normalised_parts(0, 1, nc.gpsimd)
         load_weights(3)
+        regroup_weights(2, 0, "scalar")
         regroup_weights(2, 1, "scalar")
         stat_tiles(1, 3)
-        stat_tiles(2, 0)
         aggregate(1)
+        stat_tiles(2, 0)
         project_pair(1, 0)
         layer_scales(1)
-        for i in range(GROUP):
-            merge_layers(0, i)
-        quantise_weights(2, 0, 2)
-        layer_inverse(1)
+        normalised_parts(1, 1, nc.gpsimd)
         stat_tiles(2, 1)
-        normalised_parts(0, 1)
-        normalised_parts(1, 1)
+        quantise_weights(2, 0, 2)
         project_pair(1, 1)
+        regroup_weights(3, 0, "scalar")
         stat_tiles(2, 2, 3)
         load_weights(4)
-        regroup_weights(3, 0, "scalar")
         aggregate(2)
-        spread_norm_params()
+        normalised_parts(0, 0, nc.gpsimd)
         layer_scales(2)
+        spread_norm_params()
         project_pair(2, 0)
         owed_terms()
-        layer_inverse(2)
-        normalised_parts(2, 1)
-        normalised_parts(0, 0)
-        normalised_parts(1, 0)
-        normalised_parts(2, 0)
-        regroup_weights(3, 1, "vector")
+        normalised_parts(2, 1, nc.vector)
+        for i in range(GROUP):
+            merge_layers(0, i)
+        normalised_parts(1, 0, nc.gpsimd)
+        regroup_weights(3, 1, "scalar")
         project_pair(2, 1)
         quantise_weights(3, 0, 2)
+        normalised_parts(2, 0, nc.vector)
         load_weights(5)
         for f in range(4, 7):
             norm_terms(f)
-        for n in range(1, 3):
-            for i in range(GROUP):
-                merge_layers(n, i)
+        for i in range(GROUP):
+            merge_layers(1, i)
         backs = [(n, pair) for n in range(GROUPS) for pair in range(2)]
         for n in range(3, GROUPS):
             for pair in range(2):
@@ -415,7 +407,7 @@ def tile_dcadecoderblock_pa_kernel(
                 if n + 1 < GROUPS:
                     if pair == 0:
                         regroup_weights(n + 1, 0, "vector")
-                        regroup_weights(n + 1, 1, "vector")
+                        regroup_weights(n + 1, 1, "scalar")
                     else:
                         quantise_weights(n + 1, 0, 2)
                 if n == 3:
@@ -428,8 +420,11 @@ def tile_dcadecoderblock_pa_kernel(
                         for m in range(3):
                             for i in range(GROUP):
                                 merge(m, i)
-                else:
-                    for m in range(2 if n == 4 else 3):
+                elif n == 4:
+                    for m in range(2 + pair):
                         turn_pair_back(*backs.pop(0), "scalar", "scalar")
+                else:
+                    for m in range(3 - pair):
+                        turn_pair_back(*backs.pop(0), "scalar", "vector")
         while backs:
             turn_pair_back(*backs.pop(0), "scalar", "vector")

@@ -27,7 +27,7 @@ GROUP_F = GROUP * P
 PAIR_F = 2 * P
 GROUPS = PROJ * F_TILES // GROUP
 GROUP_OF = [(n % PROJ, n // PROJ) for n in range(GROUPS)]
-BY_SCALAR = [2, 2, 1, 0, 0, 0]
+BY_SCALAR = [3, 0, 0, 0, 0, 0]
 BANK = 512
 STATS = 6
 STATS_MAX = 512
@@ -57,8 +57,8 @@ def tile_dcadecoderblock_pa_kernel(
         w_load = ctx.enter_context(tc.tile_pool(name="w_load", bufs=3))
         w_stage = ctx.enter_context(tc.tile_pool(name="w_stage", bufs=2))
         w_keep = ctx.enter_context(tc.tile_pool(name="w_keep", bufs=3))
-        norm_pool = ctx.enter_context(tc.tile_pool(name="norm", bufs=32))
-        sums = ctx.enter_context(tc.tile_pool(name="sums", bufs=20))
+        norm_pool = ctx.enter_context(tc.tile_pool(name="norm", bufs=40))
+        sums = ctx.enter_context(tc.tile_pool(name="sums", bufs=12))
         rows_pool = ctx.enter_context(tc.tile_pool(name="rows", bufs=8))
         psum_acc = ctx.enter_context(tc.psum_pool(name="psum_acc", bufs=5))
         psum_tp = ctx.enter_context(tc.psum_pool(name="psum_tp", bufs=3))
@@ -185,11 +185,11 @@ def tile_dcadecoderblock_pa_kernel(
 
         def spread_norm_params():
             spread_rows(norm_rows, norm_params)
+
+        def owed_terms():
             nc.vector.tensor_scalar_mul(
                 out=shift3[:], in0=norm_params[:, n_ft : 2 * n_ft], scalar1=float(LAYERS)
             )
-
-        def owed_terms():
             for m in set(BY_SCALAR):
                 nc.vector.scalar_tensor_tensor(
                     out=owed[m][:], in0=bias[:, 0:n_ft], scalar=float(LAYERS - m), in1=shift3[:], op0=ALU.mult, op1=ALU.add
@@ -224,7 +224,7 @@ def tile_dcadecoderblock_pa_kernel(
                 )
                 relus.setdefault(ft, []).append(relu)
             else:
-                total = relus[ft][0] if BY_SCALAR[n] else ln_term[ft]
+                total = ln_term[ft]
                 nc.vector.scalar_tensor_tensor(
                     out=total[:], in0=acc[:], scalar=neg_bias[:, ft : ft + 1], in1=total[:], op0=ALU.max, op1=ALU.add
                 )
@@ -235,6 +235,7 @@ def tile_dcadecoderblock_pa_kernel(
         mean_var = const.tile([P, n_rt, 2], F32)
         var_eps = const.tile([P, n_rt], F32)
         rstd = const.tile([P, n_rt], F32)
+        neg_mean = const.tile([P, n_rt], F32)
         z_part = {}
 
         def tile_statistics(l, j):
@@ -253,17 +254,22 @@ def tile_dcadecoderblock_pa_kernel(
                 out=var_eps[:, rts], in0=mean_var[:, rts, 1], scalar1=EPS, scalar2=0.0, op0=ALU.add, op1=ALU.add
             )
             nc.gpsimd.tensor_tensor(out=rstd[:, rts], in0=var_eps[:, rts], in1=minus_half[:], op=ALU.pow)
+            if l < LAYERS - 1:
+                nc.gpsimd.tensor_scalar(
+                    out=neg_mean[:, rts], in0=mean_var[:, rts, 0], scalar1=-1.0, scalar2=0.0, op0=ALU.mult, op1=ALU.add
+                )
 
         def normalised_parts(l, half, engine):
             for j in range(TOK_TILES):
                 rt = l * TOK_TILES + j
                 z_part[l, j, half] = norm_pool.tile([P, BANK], F32, name="z_part", tag="norm")
-                engine.tensor_scalar(
+                on_vector = engine == "vector"
+                (nc.vector if on_vector else nc.gpsimd).tensor_scalar(
                     out=z_part[l, j, half][:],
                     in0=x_sb[:, rt, half * BANK : (half + 1) * BANK],
-                    scalar1=mean_var[:, rt, 0:1],
+                    scalar1=mean_var[:, rt, 0:1] if on_vector else neg_mean[:, rt : rt + 1],
                     scalar2=rstd[:, rt : rt + 1],
-                    op0=ALU.subtract,
+                    op0=ALU.subtract if on_vector else ALU.add,
                     op1=ALU.mult,
                 )
 
@@ -295,10 +301,12 @@ def tile_dcadecoderblock_pa_kernel(
             first = relus[ft][0]
             for other in relus[ft][1:]:
                 nc.gpsimd.tensor_tensor(out=first[:], in0=first[:], in1=other[:], op=ALU.add)
+            relus[ft] = [first]
 
         def merge(n, i):
             ft = feature_tile(n, i)
-            nc.gpsimd.tensor_tensor(out=ln_term[ft][:], in0=ln_term[ft][:], in1=relus[ft][0][:], op=ALU.add)
+            for relu in relus.get(ft, []):
+                nc.gpsimd.tensor_tensor(out=ln_term[ft][:], in0=ln_term[ft][:], in1=relu[:], op=ALU.add)
 
         def turn_back(n, pair, b, engine):
             t, half = GROUP_OF[n]
@@ -342,89 +350,77 @@ def tile_dcadecoderblock_pa_kernel(
                 turn_back(n, pair, b, engines[b])
 
         turn_layer(0)
-        stat_tiles(0, 0, 1)
+        stat_tiles(0, 0, 1, 2, 3)
         turn_layer(1)
-        quantise_layer(0)
-        regroup_weights(0, 1, "scalar")
-        regroup_weights(0, 0, "vector")
-        quantise_weights(0, 0, 1)
-        quantise_layer(1)
-        quantise_weights(0, 1, 2)
-        stat_tiles(0, 2)
-        spread_biases()
-        turn_layer(2)
-        stat_tiles(0, 3)
-        project_group(0, 0)
         aggregate(0)
-        quantise_layer(2)
-        regroup_weights(1, 0, "gpsimd")
-        regroup_weights(1, 1, "vector")
+        quantise_layer(0)
+        regroup_weights(0, 0, "scalar")
         layer_scales(0)
-        project_group(0, 1)
-        stat_tiles(1, 0)
-        quantise_weights(1, 0, 2)
-        stat_tiles(1, 1, 2)
-        project_group(0, 2)
-        normalised_parts(0, 1, nc.gpsimd)
-        load_weights(3)
-        regroup_weights(2, 0, "scalar")
-        regroup_weights(2, 1, "scalar")
-        stat_tiles(1, 3)
+        normalised_parts(0, 0, "gpsimd")
+        stat_tiles(1, 0, 1)
+        quantise_layer(1)
+        turn_layer(2)
+        quantise_weights(0, 0, 1)
+        regroup_weights(0, 1, "scalar")
+        stat_tiles(1, 2, 3)
+        spread_biases()
         aggregate(1)
-        stat_tiles(2, 0)
-        project_pair(1, 0)
         layer_scales(1)
-        normalised_parts(1, 1, nc.gpsimd)
-        stat_tiles(2, 1)
-        quantise_weights(2, 0, 2)
-        project_pair(1, 1)
-        regroup_weights(3, 0, "scalar")
-        stat_tiles(2, 2, 3)
-        load_weights(4)
-        aggregate(2)
-        normalised_parts(0, 0, nc.gpsimd)
-        layer_scales(2)
+        normalised_parts(1, 0, "gpsimd")
+        quantise_weights(0, 1, 2)
+        project_group(0, 0)
+        stat_tiles(2, 0, 1)
         spread_norm_params()
-        project_pair(2, 0)
+        project_group(0, 1)
+        quantise_layer(2)
+        stat_tiles(2, 2, 3)
+        project_group(0, 2)
         owed_terms()
-        normalised_parts(2, 1, nc.vector)
+        aggregate(2)
+        layer_scales(2)
+        normalised_parts(2, 0, "vector")
+        regroup_weights(1, 1, "vector")
+        regroup_weights(1, 0, "scalar")
+        normalised_parts(0, 1, "gpsimd")
+        normalised_parts(1, 1, "gpsimd")
+        quantise_weights(1, 0, 2)
+        load_weights(3)
+        for f in range(3):
+            norm_terms(f, (1, 2, 0))
+        regroup_weights(2, 0, "vector")
+        project_pair(1, 0)
+        norm_terms(3, (1, 2, 0))
+        load_weights(4)
+        regroup_weights(2, 1, "vector")
+        quantise_weights(2, 0, 2)
+        regroup_weights(3, 0, "scalar")
+        project_pair(1, 1)
+        normalised_parts(2, 1, "vector")
         for i in range(GROUP):
             merge_layers(0, i)
-        normalised_parts(1, 0, nc.gpsimd)
-        regroup_weights(3, 1, "scalar")
-        project_pair(2, 1)
-        quantise_weights(3, 0, 2)
-        normalised_parts(2, 0, nc.vector)
-        load_weights(5)
-        for f in range(4, 7):
-            norm_terms(f)
         for i in range(GROUP):
-            merge_layers(1, i)
+            merge(0, i)
+        regroup_weights(3, 1, "scalar")
+        project_pair(2, 0)
+        load_weights(5)
+        quantise_weights(3, 0, 2)
+        regroup_weights(4, 0, "scalar")
+        for f in range(4, 6):
+            norm_terms(f)
+        project_pair(2, 1)
+        for f in range(6, 8):
+            norm_terms(f)
         backs = [(n, pair) for n in range(GROUPS) for pair in range(2)]
         for n in range(3, GROUPS):
             for pair in range(2):
                 project_pair(n, pair)
-                if n + 1 < GROUPS:
-                    if pair == 0:
-                        regroup_weights(n + 1, 0, "vector")
-                        regroup_weights(n + 1, 1, "scalar")
-                    else:
-                        quantise_weights(n + 1, 0, 2)
+                if n + 1 < GROUPS and pair == 1:
+                    quantise_weights(n + 1, 0, 2)
+                for m in range(2 if n < 5 or pair else 1):
+                    turn_pair_back(*backs.pop(0), "scalar", "scalar")
                 if n == 3:
-                    if pair == 0:
-                        norm_terms(7)
-                        norm_terms(0)
-                    else:
-                        for f in range(1, 4):
-                            norm_terms(f)
-                        for m in range(3):
-                            for i in range(GROUP):
-                                merge(m, i)
-                elif n == 4:
-                    for m in range(2 + pair):
-                        turn_pair_back(*backs.pop(0), "scalar", "scalar")
-                else:
-                    for m in range(3 - pair):
-                        turn_pair_back(*backs.pop(0), "scalar", "vector")
+                    regroup_weights(4 + pair, 1 - pair, "vector" if pair == 0 else "scalar")
+                if n == 4 and pair == 0:
+                    regroup_weights(5, 1, "scalar")
         while backs:
             turn_pair_back(*backs.pop(0), "scalar", "vector")

@@ -68,10 +68,10 @@ def tile_dcadecoderblock_pa_kernel(
         make_identity(nc, ident_f32[:])
         ident_bf16 = const.tile([P, P], BF16)
         make_identity(nc, ident_bf16[:])
-        minus_half = const.tile([P, TOK_TILES], F32)
-        nc.vector.memset(minus_half[:], -0.5)
+        eps = const.tile([P, 1], F32)
+        nc.vector.memset(eps[:], EPS)
         table_warm = const.tile([P, 1], F32)
-        nc.scalar.activation(out=table_warm[:], in_=minus_half[:, 0:1], func=ACT.Relu)
+        nc.scalar.activation(out=table_warm[:], in_=eps[:], func=ACT.Sqrt)
         bias_rows = const.tile([P, P], BF16)
         norm_rows = const.tile([P, P], BF16)
         nc.vector.memset(bias_rows[:], 0.0)
@@ -150,12 +150,8 @@ def tile_dcadecoderblock_pa_kernel(
             src = w_raw[n][:, g, :, :].rearrange("p t (c i) -> p c t i", i=4)
             if engine == "vector":
                 nc.vector.tensor_copy(out=dst, in_=src)
-            elif engine == "scalar":
-                nc.scalar.copy(out=dst, in_=src)
             else:
-                dst = w_grouped[n][:, g, :, :]
-                src = w_raw[n][:, g, :, :].rearrange("p t c -> p c t")
-                nc.gpsimd.tensor_scalar(out=dst, in0=src, scalar1=1.0, scalar2=0.0, op0=ALU.mult, op1=ALU.add)
+                nc.scalar.copy(out=w_grouped[n][:, g, :, :], in_=w_raw[n][:, g, :, :].rearrange("p t c -> p c t"))
 
         def quantise_weights(n, g_from, g_to):
             if g_from == 0:
@@ -233,7 +229,7 @@ def tile_dcadecoderblock_pa_kernel(
         chunks = DIM // STATS_MAX
         stats = const.tile([P, n_rt, chunks, STATS], F32)
         mean_var = const.tile([P, n_rt, 2], F32)
-        var_eps = const.tile([P, n_rt], F32)
+        std = const.tile([P, n_rt], F32)
         rstd = const.tile([P, n_rt], F32)
         neg_mean = const.tile([P, n_rt], F32)
         z_part = {}
@@ -250,14 +246,12 @@ def tile_dcadecoderblock_pa_kernel(
 
         def layer_scales(l):
             rts = slice(l * TOK_TILES, (l + 1) * TOK_TILES)
-            nc.gpsimd.tensor_scalar(
-                out=var_eps[:, rts], in0=mean_var[:, rts, 1], scalar1=EPS, scalar2=0.0, op0=ALU.add, op1=ALU.add
-            )
-            nc.gpsimd.tensor_tensor(out=rstd[:, rts], in0=var_eps[:, rts], in1=minus_half[:], op=ALU.pow)
-            if l < LAYERS - 1:
-                nc.gpsimd.tensor_scalar(
-                    out=neg_mean[:, rts], in0=mean_var[:, rts, 0], scalar1=-1.0, scalar2=0.0, op0=ALU.mult, op1=ALU.add
-                )
+            nc.scalar.activation(out=std[:, rts], in_=mean_var[:, rts, 1], func=ACT.Sqrt, bias=eps[:, 0:1], scale=1.0)
+            nc.vector.tensor_scalar_mul(out=neg_mean[:, rts], in0=mean_var[:, rts, 0], scalar1=-1.0)
+
+        def layer_inverse(l):
+            rts = slice(l * TOK_TILES, (l + 1) * TOK_TILES)
+            nc.vector.reciprocal(out=rstd[:, rts], in_=std[:, rts])
 
         def normalised_parts(l, half, engine):
             for j in range(TOK_TILES):
@@ -356,8 +350,10 @@ def tile_dcadecoderblock_pa_kernel(
         quantise_layer(0)
         regroup_weights(0, 0, "scalar")
         layer_scales(0)
+        stat_tiles(1, 0)
+        layer_inverse(0)
         normalised_parts(0, 0, "gpsimd")
-        stat_tiles(1, 0, 1)
+        stat_tiles(1, 1)
         quantise_layer(1)
         turn_layer(2)
         quantise_weights(0, 0, 1)
@@ -366,8 +362,9 @@ def tile_dcadecoderblock_pa_kernel(
         spread_biases()
         aggregate(1)
         layer_scales(1)
-        normalised_parts(1, 0, "gpsimd")
         quantise_weights(0, 1, 2)
+        layer_inverse(1)
+        normalised_parts(1, 0, "gpsimd")
         project_group(0, 0)
         stat_tiles(2, 0, 1)
         spread_norm_params()
@@ -378,6 +375,7 @@ def tile_dcadecoderblock_pa_kernel(
         owed_terms()
         aggregate(2)
         layer_scales(2)
+        layer_inverse(2)
         normalised_parts(2, 0, "vector")
         regroup_weights(1, 1, "vector")
         regroup_weights(1, 0, "scalar")

@@ -119,6 +119,14 @@ def tile_dcadecoderblock_pa_kernel(
         x_scales = const.tile([P, LAYERS * K_PASSES * TOK], U8, align_bytes=64)
         grouped = {}
 
+        idle_cols = const.tile([P, BANK], BF16)
+        nc.gpsimd.memset(idle_cols[:], 0.0)
+        idle_bank = psum_acc.tile([P, BANK], F32, tag="acc", name="idle_bank")
+
+        def keep_warm(count):
+            for k in range(count):
+                nc.tensor.matmul(out=idle_bank[:], lhsT=ident_bf16[:], rhs=idle_cols[:], start=True, stop=True)
+
         def turn_tokens(l, j):
             if j == 0:
                 grouped[l] = x_stage.tile([P, K_PASSES * TOK * PACK], BF16, align_bytes=64, name="grouped")
@@ -329,39 +337,50 @@ def tile_dcadecoderblock_pa_kernel(
         def turn_layer(l):
             for j in range(TOK_TILES):
                 turn_tokens(l, j)
+                keep_warm(1)
 
         def project_group(n, l):
             for i in range(GROUP):
                 project(n, i, l)
 
-        def project_pair(n, pair):
-            for l in range(LAYERS):
-                for i in (2 * pair, 2 * pair + 1):
-                    project(n, i, l)
+        def project_pair(n, pair, *between):
+            for k in range(2 * LAYERS):
+                l, e = divmod(k, 2)
+                project(n, 2 * pair + e, l)
+                if k % LAYERS == LAYERS - 1 and k // LAYERS < len(between):
+                    between[k // LAYERS]()
 
         def turn_pair_back(n, pair, *engines):
             for b in range(BATCH):
                 turn_back(n, pair, b, engines[b])
 
+        def norm_run(f, ts=range(PROJ)):
+            return lambda: norm_terms(f, ts)
+
+        def back_run(n, pair, *engines):
+            return lambda: turn_pair_back(n, pair, *engines)
+
+        keep_warm(8)
         turn_layer(0)
         stat_tiles(0, 0, 1, 2, 3)
         turn_layer(1)
         aggregate(0)
+        layer_scales(0)
         quantise_layer(0)
         regroup_weights(0, 0, "scalar")
-        layer_scales(0)
         stat_tiles(1, 0)
         layer_inverse(0)
         normalised_parts(0, 0, "gpsimd")
         stat_tiles(1, 1)
         quantise_layer(1)
-        turn_layer(2)
         quantise_weights(0, 0, 1)
-        regroup_weights(0, 1, "scalar")
         stat_tiles(1, 2, 3)
+        turn_layer(2)
+        regroup_weights(0, 1, "scalar")
         spread_biases()
         aggregate(1)
         layer_scales(1)
+        keep_warm(4)
         quantise_weights(0, 1, 2)
         layer_inverse(1)
         normalised_parts(1, 0, "gpsimd")
@@ -371,54 +390,50 @@ def tile_dcadecoderblock_pa_kernel(
         project_group(0, 1)
         quantise_layer(2)
         stat_tiles(2, 2, 3)
-        project_group(0, 2)
-        owed_terms()
         aggregate(2)
         layer_scales(2)
+        owed_terms()
         layer_inverse(2)
         normalised_parts(2, 0, "vector")
-        regroup_weights(1, 1, "vector")
-        regroup_weights(1, 0, "scalar")
         normalised_parts(0, 1, "gpsimd")
         normalised_parts(1, 1, "gpsimd")
+        regroup_weights(1, 1, "vector")
+        regroup_weights(1, 0, "scalar")
+        project(0, 0, 2)
+        project(0, 1, 2)
+        norm_terms(0, (1, 2, 0))
         quantise_weights(1, 0, 2)
+        project(0, 2, 2)
+        project(0, 3, 2)
+        norm_terms(1, (1, 2, 0))
         load_weights(3)
-        for f in range(3):
-            norm_terms(f, (1, 2, 0))
+        normalised_parts(2, 1, "vector")
         regroup_weights(2, 0, "vector")
-        project_pair(1, 0)
-        norm_terms(3, (1, 2, 0))
+        project_pair(1, 0, norm_run(2, (1, 2, 0)), norm_run(3, (1, 2, 0)))
         load_weights(4)
         regroup_weights(2, 1, "vector")
         quantise_weights(2, 0, 2)
-        regroup_weights(3, 0, "scalar")
-        project_pair(1, 1)
-        normalised_parts(2, 1, "vector")
+        project_pair(1, 1, norm_run(4), norm_run(5))
         for i in range(GROUP):
             merge_layers(0, i)
         for i in range(GROUP):
             merge(0, i)
-        regroup_weights(3, 1, "scalar")
-        project_pair(2, 0)
+        regroup_weights(3, 0, "scalar")
+        project_pair(2, 0, norm_run(6), norm_run(7))
         load_weights(5)
+        regroup_weights(3, 1, "vector")
         quantise_weights(3, 0, 2)
+        project_pair(2, 1, back_run(0, 0, "scalar", "scalar"), back_run(0, 1, "scalar", "scalar"))
         regroup_weights(4, 0, "scalar")
-        for f in range(4, 6):
-            norm_terms(f)
-        project_pair(2, 1)
-        for f in range(6, 8):
-            norm_terms(f)
-        backs = [(n, pair) for n in range(GROUPS) for pair in range(2)]
-        for n in range(3, GROUPS):
-            for pair in range(2):
-                project_pair(n, pair)
-                if n + 1 < GROUPS and pair == 1:
-                    quantise_weights(n + 1, 0, 2)
-                for m in range(2 if n < 5 or pair else 1):
-                    turn_pair_back(*backs.pop(0), "scalar", "scalar")
-                if n == 3:
-                    regroup_weights(4 + pair, 1 - pair, "vector" if pair == 0 else "scalar")
-                if n == 4 and pair == 0:
-                    regroup_weights(5, 1, "scalar")
-        while backs:
-            turn_pair_back(*backs.pop(0), "scalar", "vector")
+        project_pair(3, 0, back_run(1, 0, "scalar", "scalar"), back_run(1, 1, "scalar", "scalar"))
+        regroup_weights(4, 1, "vector")
+        quantise_weights(4, 0, 2)
+        regroup_weights(5, 0, "scalar")
+        project_pair(3, 1, back_run(2, 0, "scalar", "scalar"), back_run(2, 1, "scalar", "scalar"))
+        regroup_weights(5, 1, "scalar")
+        project_pair(4, 0, back_run(3, 0, "scalar", "scalar"))
+        quantise_weights(5, 0, 2)
+        project_pair(4, 1, back_run(3, 1, "scalar", "scalar"))
+        project_pair(5, 0, back_run(4, 0, "scalar", "scalar"))
+        project_pair(5, 1, back_run(4, 1, "scalar", "scalar"), back_run(5, 0, "scalar", "vector"))
+        turn_pair_back(5, 1, "scalar", "vector")

@@ -68,10 +68,10 @@ def tile_dcadecoderblock_pa_kernel(
         make_identity(nc, ident_f32[:])
         ident_bf16 = const.tile([P, P], BF16)
         make_identity(nc, ident_bf16[:])
-        eps = const.tile([P, 1], F32)
-        nc.vector.memset(eps[:], EPS)
+        minus_half = const.tile([P, TOK_TILES], F32)
+        nc.vector.memset(minus_half[:], -0.5)
         table_warm = const.tile([P, 1], F32)
-        nc.scalar.activation(out=table_warm[:], in_=eps[:], func=ACT.Sqrt)
+        nc.scalar.activation(out=table_warm[:], in_=minus_half[:, 0:1], func=ACT.Relu)
         bias_rows = const.tile([P, P], BF16)
         norm_rows = const.tile([P, P], BF16)
         nc.vector.memset(bias_rows[:], 0.0)
@@ -118,14 +118,6 @@ def tile_dcadecoderblock_pa_kernel(
         x_codes = const.tile([P, LAYERS * K_PASSES * TOK], U32, align_bytes=64)
         x_scales = const.tile([P, LAYERS * K_PASSES * TOK], U8, align_bytes=64)
         grouped = {}
-
-        idle_cols = const.tile([P, BANK], BF16)
-        nc.gpsimd.memset(idle_cols[:], 0.0)
-        idle_bank = psum_acc.tile([P, BANK], F32, tag="acc", name="idle_bank")
-
-        def keep_warm(count):
-            for k in range(count):
-                nc.tensor.matmul(out=idle_bank[:], lhsT=ident_bf16[:], rhs=idle_cols[:], start=True, stop=True)
 
         def turn_tokens(l, j):
             if j == 0:
@@ -185,12 +177,12 @@ def tile_dcadecoderblock_pa_kernel(
 
         def spread_biases():
             spread_rows(bias_rows, bias)
-            nc.vector.tensor_scalar_mul(out=neg_bias[:], in0=bias[:, 0:n_ft], scalar1=-1.0)
 
         def spread_norm_params():
             spread_rows(norm_rows, norm_params)
 
         def owed_terms():
+            nc.vector.tensor_scalar_mul(out=neg_bias[:], in0=bias[:, 0:n_ft], scalar1=-1.0)
             nc.vector.tensor_scalar_mul(
                 out=shift3[:], in0=norm_params[:, n_ft : 2 * n_ft], scalar1=float(LAYERS)
             )
@@ -237,7 +229,7 @@ def tile_dcadecoderblock_pa_kernel(
         chunks = DIM // STATS_MAX
         stats = const.tile([P, n_rt, chunks, STATS], F32)
         mean_var = const.tile([P, n_rt, 2], F32)
-        std = const.tile([P, n_rt], F32)
+        var_eps = const.tile([P, n_rt], F32)
         rstd = const.tile([P, n_rt], F32)
         neg_mean = const.tile([P, n_rt], F32)
         z_part = {}
@@ -254,12 +246,14 @@ def tile_dcadecoderblock_pa_kernel(
 
         def layer_scales(l):
             rts = slice(l * TOK_TILES, (l + 1) * TOK_TILES)
-            nc.scalar.activation(out=std[:, rts], in_=mean_var[:, rts, 1], func=ACT.Sqrt, bias=eps[:, 0:1], scale=1.0)
-            nc.vector.tensor_scalar_mul(out=neg_mean[:, rts], in0=mean_var[:, rts, 0], scalar1=-1.0)
-
-        def layer_inverse(l):
-            rts = slice(l * TOK_TILES, (l + 1) * TOK_TILES)
-            nc.vector.reciprocal(out=rstd[:, rts], in_=std[:, rts])
+            nc.gpsimd.tensor_scalar(
+                out=var_eps[:, rts], in0=mean_var[:, rts, 1], scalar1=EPS, scalar2=0.0, op0=ALU.add, op1=ALU.add
+            )
+            nc.gpsimd.tensor_tensor(out=rstd[:, rts], in0=var_eps[:, rts], in1=minus_half[:], op=ALU.pow)
+            if l < LAYERS - 1:
+                nc.gpsimd.tensor_scalar(
+                    out=neg_mean[:, rts], in0=mean_var[:, rts, 0], scalar1=-1.0, scalar2=0.0, op0=ALU.mult, op1=ALU.add
+                )
 
         def normalised_parts(l, half, engine):
             for j in range(TOK_TILES):
@@ -337,7 +331,6 @@ def tile_dcadecoderblock_pa_kernel(
         def turn_layer(l):
             for j in range(TOK_TILES):
                 turn_tokens(l, j)
-                keep_warm(1)
 
         def project_group(n, l):
             for i in range(GROUP):
@@ -360,40 +353,33 @@ def tile_dcadecoderblock_pa_kernel(
         def back_run(n, pair, *engines):
             return lambda: turn_pair_back(n, pair, *engines)
 
-        keep_warm(8)
         turn_layer(0)
         stat_tiles(0, 0, 1, 2, 3)
         turn_layer(1)
         aggregate(0)
         layer_scales(0)
-        quantise_layer(0)
         regroup_weights(0, 0, "scalar")
-        stat_tiles(1, 0)
-        layer_inverse(0)
+        stat_tiles(1, 0, 1, 2, 3)
+        quantise_layer(0)
         normalised_parts(0, 0, "gpsimd")
-        stat_tiles(1, 1)
-        quantise_layer(1)
-        quantise_weights(0, 0, 1)
-        stat_tiles(1, 2, 3)
-        turn_layer(2)
         regroup_weights(0, 1, "scalar")
-        spread_biases()
         aggregate(1)
         layer_scales(1)
-        keep_warm(4)
-        quantise_weights(0, 1, 2)
-        layer_inverse(1)
+        quantise_layer(1)
+        turn_layer(2)
+        spread_biases()
+        stat_tiles(2, 0)
+        quantise_weights(0, 0, 2)
         normalised_parts(1, 0, "gpsimd")
+        stat_tiles(2, 1)
         project_group(0, 0)
-        stat_tiles(2, 0, 1)
         spread_norm_params()
-        project_group(0, 1)
         quantise_layer(2)
+        project_group(0, 1)
         stat_tiles(2, 2, 3)
         aggregate(2)
         layer_scales(2)
         owed_terms()
-        layer_inverse(2)
         normalised_parts(2, 0, "vector")
         normalised_parts(0, 1, "gpsimd")
         normalised_parts(1, 1, "gpsimd")

@@ -68,10 +68,11 @@ def tile_dcadecoderblock_pa_kernel(
         make_identity(nc, ident_f32[:])
         ident_bf16 = const.tile([P, P], BF16)
         make_identity(nc, ident_bf16[:])
-        minus_half = const.tile([P, TOK_TILES], F32)
-        nc.vector.memset(minus_half[:], -0.5)
+        eps = const.tile([P, 1], F32)
+        nc.vector.memset(eps[:], 0.0)
+        nc.vector.tensor_scalar_add(out=eps[:], in0=eps[:], scalar1=EPS)
         table_warm = const.tile([P, 1], F32)
-        nc.scalar.activation(out=table_warm[:], in_=minus_half[:, 0:1], func=ACT.Relu)
+        nc.scalar.activation(out=table_warm[:], in_=eps[:], func=ACT.Abs_reciprocal_sqrt)
         bias_rows = const.tile([P, P], BF16)
         norm_rows = const.tile([P, P], BF16)
         nc.vector.memset(bias_rows[:], 0.0)
@@ -82,10 +83,12 @@ def tile_dcadecoderblock_pa_kernel(
         def load_layer(l):
             for b in range(BATCH):
                 rt = l * TOK_TILES + 2 * b
-                nc.sync.dma_start(
-                    out=x_sb[:, rt : rt + 2, :],
-                    in_=layer_outputs[b, l, :, :].rearrange("(h p) d -> p h d", p=P),
-                )
+                tokens = layer_outputs[b, l, :, :].rearrange("(p h) d -> p h d", p=P)
+                if l == 0 and b == 0:
+                    nc.sync.dma_start(out=x_sb[:, rt, :], in_=tokens[:, 0, :])
+                    nc.sync.dma_start(out=x_sb[:, rt + 1, :], in_=tokens[:, 1, :])
+                else:
+                    nc.sync.dma_start(out=x_sb[:, rt : rt + 2, :], in_=tokens)
 
         w_raw = {}
 
@@ -150,6 +153,11 @@ def tile_dcadecoderblock_pa_kernel(
             src = w_raw[n][:, g, :, :].rearrange("p t (c i) -> p c t i", i=4)
             if engine == "vector":
                 nc.vector.tensor_copy(out=dst, in_=src)
+            elif engine == "gpsimd":
+                nc.gpsimd.tensor_scalar(
+                    out=w_grouped[n][:, g, :, :], in0=w_raw[n][:, g, :, :].rearrange("p t c -> p c t"),
+                    scalar1=1.0, scalar2=0.0, op0=ALU.mult, op1=ALU.add,
+                )
             else:
                 nc.scalar.copy(out=w_grouped[n][:, g, :, :], in_=w_raw[n][:, g, :, :].rearrange("p t c -> p c t"))
 
@@ -229,7 +237,6 @@ def tile_dcadecoderblock_pa_kernel(
         chunks = DIM // STATS_MAX
         stats = const.tile([P, n_rt, chunks, STATS], F32)
         mean_var = const.tile([P, n_rt, 2], F32)
-        var_eps = const.tile([P, n_rt], F32)
         rstd = const.tile([P, n_rt], F32)
         neg_mean = const.tile([P, n_rt], F32)
         z_part = {}
@@ -246,10 +253,9 @@ def tile_dcadecoderblock_pa_kernel(
 
         def layer_scales(l):
             rts = slice(l * TOK_TILES, (l + 1) * TOK_TILES)
-            nc.gpsimd.tensor_scalar(
-                out=var_eps[:, rts], in0=mean_var[:, rts, 1], scalar1=EPS, scalar2=0.0, op0=ALU.add, op1=ALU.add
+            nc.scalar.activation(
+                out=rstd[:, rts], in_=mean_var[:, rts, 1], func=ACT.Abs_reciprocal_sqrt, bias=eps[:, 0:1], scale=1.0
             )
-            nc.gpsimd.tensor_tensor(out=rstd[:, rts], in0=var_eps[:, rts], in1=minus_half[:], op=ALU.pow)
             if l < LAYERS - 1:
                 nc.gpsimd.tensor_scalar(
                     out=neg_mean[:, rts], in0=mean_var[:, rts, 0], scalar1=-1.0, scalar2=0.0, op0=ALU.mult, op1=ALU.add
@@ -321,8 +327,26 @@ def tile_dcadecoderblock_pa_kernel(
                 nc.scalar.copy(out=rows[:], in_=back[:])
             f0 = half * GROUP_F + pair * PAIR_F
             nc.sync.dma_start(
-                out=outs[t][b, :, f0 : f0 + PAIR_F].rearrange("(h p) f -> p h f", p=P), in_=rows[:]
+                out=outs[t][b, :, f0 : f0 + PAIR_F].rearrange("(p h) f -> p h f", p=P), in_=rows[:]
             )
+
+        def turn_one_back(n, i):
+            t, half = GROUP_OF[n]
+            ft = feature_tile(n, i)
+            f0 = half * GROUP_F + i * P
+            for b in range(BATCH):
+                back = psum_tp.tile([P, SEQ // P, P], F32, tag="tp", name="back")
+                for h in range(SEQ // P):
+                    j = b * (SEQ // P) + h
+                    nc.tensor.transpose(back[:, h, :], ln_term[ft][:, j * P : (j + 1) * P], ident_f32[:])
+                rows = rows_pool.tile([P, SEQ // P, P], F32, name="rows")
+                if b == 0:
+                    nc.scalar.copy(out=rows[:], in_=back[:])
+                else:
+                    nc.vector.tensor_copy(out=rows[:], in_=back[:])
+                nc.sync.dma_start(
+                    out=outs[t][b, :, f0 : f0 + P].rearrange("(p h) f -> p h f", p=P), in_=rows[:]
+                )
 
         def stat_tiles(l, *js):
             for j in js:
@@ -371,20 +395,20 @@ def tile_dcadecoderblock_pa_kernel(
         stat_tiles(2, 0)
         quantise_weights(0, 0, 2)
         normalised_parts(1, 0, "gpsimd")
+        regroup_weights(1, 0, "gpsimd")
         stat_tiles(2, 1)
         project_group(0, 0)
         spread_norm_params()
         quantise_layer(2)
-        project_group(0, 1)
         stat_tiles(2, 2, 3)
         aggregate(2)
         layer_scales(2)
+        project_group(0, 1)
         owed_terms()
         normalised_parts(2, 0, "vector")
         normalised_parts(0, 1, "gpsimd")
         normalised_parts(1, 1, "gpsimd")
         regroup_weights(1, 1, "vector")
-        regroup_weights(1, 0, "scalar")
         project(0, 0, 2)
         project(0, 1, 2)
         norm_terms(0, (1, 2, 0))
@@ -421,5 +445,12 @@ def tile_dcadecoderblock_pa_kernel(
         quantise_weights(5, 0, 2)
         project_pair(4, 1, back_run(3, 1, "scalar", "scalar"))
         project_pair(5, 0, back_run(4, 0, "scalar", "scalar"))
-        project_pair(5, 1, back_run(4, 1, "scalar", "scalar"), back_run(5, 0, "scalar", "vector"))
-        turn_pair_back(5, 1, "scalar", "vector")
+        for l in range(LAYERS):
+            project(5, 2, l)
+        turn_pair_back(4, 1, "scalar", "scalar")
+        project(5, 3, 0)
+        project(5, 3, 1)
+        turn_pair_back(5, 0, "scalar", "scalar")
+        turn_one_back(5, 2)
+        project(5, 3, 2)
+        turn_one_back(5, 3)

@@ -122,6 +122,14 @@ def tile_dcadecoderblock_pa_kernel(
         x_scales = const.tile([P, LAYERS * K_PASSES * TOK], U8, align_bytes=64)
         grouped = {}
 
+        idle_cols = const.tile([P, BANK], BF16)
+        nc.vector.memset(idle_cols[:], 0.0)
+        idle_bank = psum_acc.tile([P, BANK], F32, tag="acc", name="idle_bank")
+
+        def keep_warm(count):
+            for k in range(count):
+                nc.tensor.matmul(out=idle_bank[:], lhsT=idle_cols[:, 0:P], rhs=idle_cols[:], start=True, stop=True)
+
         def turn_tokens(l, j):
             if j == 0:
                 grouped[l] = x_stage.tile([P, K_PASSES * TOK * PACK], BF16, align_bytes=64, name="grouped")
@@ -355,6 +363,7 @@ def tile_dcadecoderblock_pa_kernel(
         def turn_layer(l):
             for j in range(TOK_TILES):
                 turn_tokens(l, j)
+                keep_warm(2)
 
         def project_group(n, l):
             for i in range(GROUP):
@@ -377,12 +386,13 @@ def tile_dcadecoderblock_pa_kernel(
         def back_run(n, pair, *engines):
             return lambda: turn_pair_back(n, pair, *engines)
 
+        keep_warm(8)
         turn_layer(0)
         stat_tiles(0, 0, 1, 2, 3)
         turn_layer(1)
         aggregate(0)
         layer_scales(0)
-        regroup_weights(0, 0, "scalar")
+        regroup_weights(0, 0, "gpsimd")
         stat_tiles(1, 0, 1, 2, 3)
         quantise_layer(0)
         normalised_parts(0, 0, "gpsimd")
@@ -397,6 +407,7 @@ def tile_dcadecoderblock_pa_kernel(
         normalised_parts(1, 0, "gpsimd")
         regroup_weights(1, 0, "gpsimd")
         stat_tiles(2, 1)
+        keep_warm(3)
         project_group(0, 0)
         spread_norm_params()
         quantise_layer(2)
@@ -433,9 +444,9 @@ def tile_dcadecoderblock_pa_kernel(
         load_weights(5)
         regroup_weights(3, 1, "vector")
         quantise_weights(3, 0, 2)
-        project_pair(2, 1, back_run(0, 0, "scalar", "scalar"), back_run(0, 1, "scalar", "scalar"))
+        project_pair(2, 1, back_run(1, 0, "scalar", "scalar"), back_run(1, 1, "scalar", "scalar"))
         regroup_weights(4, 0, "scalar")
-        project_pair(3, 0, back_run(1, 0, "scalar", "scalar"), back_run(1, 1, "scalar", "scalar"))
+        project_pair(3, 0, back_run(0, 0, "scalar", "scalar"), back_run(0, 1, "scalar", "scalar"))
         regroup_weights(4, 1, "vector")
         quantise_weights(4, 0, 2)
         regroup_weights(5, 0, "scalar")

from contextlib import ExitStack

import concourse.mybir as mybir
from concourse.masks import make_identity

F32 = mybir.dt.float32
BF16 = mybir.dt.bfloat16
U32 = mybir.dt.uint32
U8 = mybir.dt.uint8
FP8X4 = mybir.dt.float8_e4m3fn_x4
ACT = mybir.ActivationFunctionType
ALU = mybir.AluOpType

P = 128
PACK = 4
K_PASS = P * PACK

BATCH, LAYERS, SEQ, DIM = 2, 3, 256, 1024
EPS = 1e-5
PROJ = 3
K_PASSES = DIM // K_PASS
TOK = BATCH * SEQ
TOK_TILES = TOK // P
F_TILES = DIM // P
GROUP = 4
GROUP_F = GROUP * P
PAIR_F = 2 * P
GROUPS = PROJ * F_TILES // GROUP
GROUP_OF = [(n % PROJ, n // PROJ) for n in range(GROUPS)]
BY_SCALAR = [3, 0, 0, 0, 0, 0]
BANK = 512
STATS = 6
STATS_MAX = 512

FLOPS = 2 * BATCH * LAYERS * SEQ * DIM * PROJ * DIM


def tile_dcadecoderblock_pa_kernel(
    tc,
    layer_outputs,
    grn_q_W, grn_q_b, grn_q_g, grn_q_be,
    grn_k_W, grn_k_b, grn_k_g, grn_k_be,
    grn_v_W, grn_v_b, grn_v_g, grn_v_be,
    out_0, out_1, out_2,
):
    nc = tc.nc
    weights = [grn_q_W, grn_k_W, grn_v_W]
    outs = [out_0, out_1, out_2]
    biases = [grn_q_b, grn_k_b, grn_v_b]
    gains = [grn_q_g, grn_k_g, grn_v_g]
    shifts = [grn_q_be, grn_k_be, grn_v_be]
    n_ft = PROJ * F_TILES

    with ExitStack() as ctx:
        const = ctx.enter_context(tc.tile_pool(name="const", bufs=1))
        x_stage = ctx.enter_context(tc.tile_pool(name="x_stage", bufs=2))
        w_load = ctx.enter_context(tc.tile_pool(name="w_load", bufs=3))
        w_stage = ctx.enter_context(tc.tile_pool(name="w_stage", bufs=2))
        w_keep = ctx.enter_context(tc.tile_pool(name="w_keep", bufs=3))
        norm_pool = ctx.enter_context(tc.tile_pool(name="norm", bufs=40))
        sums = ctx.enter_context(tc.tile_pool(name="sums", bufs=12))
        rows_pool = ctx.enter_context(tc.tile_pool(name="rows", bufs=8))
        psum_acc = ctx.enter_context(tc.psum_pool(name="psum_acc", bufs=5))
        psum_tp = ctx.enter_context(tc.psum_pool(name="psum_tp", bufs=3))
        ctx.enter_context(tc.manual_schedule())

        ident_f32 = const.tile([P, P], F32)
        make_identity(nc, ident_f32[:])
        ident_bf16 = const.tile([P, P], BF16)
        make_identity(nc, ident_bf16[:])
        eps = const.tile([P, 1], F32)
        nc.vector.memset(eps[:], 0.0)
        nc.vector.tensor_scalar_add(out=eps[:], in0=eps[:], scalar1=EPS)
        table_warm = const.tile([P, 1], F32)
        nc.scalar.activation(out=table_warm[:], in_=eps[:], func=ACT.Abs_reciprocal_sqrt)
        bias_rows = const.tile([P, P], BF16)
        norm_rows = const.tile([P, P], BF16)
        nc.vector.memset(bias_rows[:], 0.0)
        nc.vector.memset(norm_rows[:], 0.0)

        x_sb = const.tile([P, LAYERS * TOK_TILES, DIM], BF16)

        def load_layer(l):
            for b in range(BATCH):
                rt = l * TOK_TILES + 2 * b
                tokens = layer_outputs[b, l, :, :].rearrange("(p h) d -> p h d", p=P)
                if l == 0 and b == 0:
                    nc.sync.dma_start(out=x_sb[:, rt, :], in_=tokens[:, 0, :])
                    nc.sync.dma_start(out=x_sb[:, rt + 1, :], in_=tokens[:, 1, :])
                else:
                    nc.sync.dma_start(out=x_sb[:, rt : rt + 2, :], in_=tokens)

        w_raw = {}

        def load_weights(n):
            t, half = GROUP_OF[n]
            w_raw[n] = w_load.tile([P, K_PASSES, PACK, GROUP_F], BF16, name="w_raw")
            for g in range(K_PASSES):
                nc.sync.dma_start(
                    out=w_raw[n][:, g, :, :],
                    in_=weights[t][g * K_PASS : (g + 1) * K_PASS, half * GROUP_F : (half + 1) * GROUP_F].rearrange(
                        "(p j) c -> p j c", j=PACK
                    ),
                )

        def load_vectors(rows, vecs):
            for v, vec in enumerate(vecs):
                nc.sync.dma_start(
                    out=rows[v * F_TILES : (v + 1) * F_TILES, :], in_=vec.rearrange("(r c) -> r c", c=P)
                )

        load_layer(0)
        load_layer(1)
        load_weights(0)
        load_vectors(bias_rows, biases)
        load_layer(2)
        load_weights(1)
        load_vectors(norm_rows, gains + shifts)
        load_weights(2)

        x_codes = const.tile([P, LAYERS * K_PASSES * TOK], U32, align_bytes=64)
        x_scales = const.tile([P, LAYERS * K_PASSES * TOK], U8, align_bytes=64)
        grouped = {}

        idle_cols = const.tile([P, BANK], BF16)
        nc.vector.memset(idle_cols[:], 0.0)
        idle_bank = psum_acc.tile([P, BANK], F32, tag="acc", name="idle_bank")

        def keep_warm(count):
            for k in range(count):
                nc.tensor.matmul(out=idle_bank[:], lhsT=idle_cols[:, 0:P], rhs=idle_cols[:], start=True, stop=True)

        def turn_tokens(l, j):
            if j == 0:
                grouped[l] = x_stage.tile([P, K_PASSES * TOK * PACK], BF16, align_bytes=64, name="grouped")
            grouped_words = grouped[l][:].bitcast(F32).rearrange("p (g r u) -> p g r u", g=K_PASSES, u=2)
            x_words = x_sb[:, l * TOK_TILES + j, :].bitcast(F32)
            xt = psum_tp.tile([P, BANK], F32, tag="tp", name="xt")
            for gu in range(BANK // P):
                g, u = divmod(gu, 2)
                nc.tensor.transpose(
                    xt[:, gu * P : (gu + 1) * P], x_words[:, 2 * P * g + u : 2 * P * (g + 1) : 2], ident_f32[:]
                )
            nc.scalar.copy(
                out=grouped_words[:, :, j * P : (j + 1) * P, :],
                in_=xt[:].rearrange("p (g u r) -> p g r u", g=K_PASSES, u=2),
            )

        def quantise_layer(l):
            cols = slice(l * K_PASSES * TOK, (l + 1) * K_PASSES * TOK)
            nc.vector.quantize_mx(out=x_codes[:, cols].bitcast(FP8X4), scales=x_scales[:, cols], in_=grouped[l][:])

        w_grouped = {}
        w_codes = {}
        w_scales = {}

        def regroup_weights(n, g, engine):
            if n not in w_grouped:
                w_grouped[n] = w_stage.tile([P, K_PASSES, GROUP_F, PACK], BF16, align_bytes=64, name="w_grouped")
            dst = w_grouped[n][:, g, :, :].rearrange("p (c i) t -> p c t i", i=4)
            src = w_raw[n][:, g, :, :].rearrange("p t (c i) -> p c t i", i=4)
            if engine == "vector":
                nc.vector.tensor_copy(out=dst, in_=src)
            elif engine == "gpsimd":
                nc.gpsimd.tensor_scalar(
                    out=w_grouped[n][:, g, :, :], in0=w_raw[n][:, g, :, :].rearrange("p t c -> p c t"),
                    scalar1=1.0, scalar2=0.0, op0=ALU.mult, op1=ALU.add,
                )
            else:
                nc.scalar.copy(out=w_grouped[n][:, g, :, :], in_=w_raw[n][:, g, :, :].rearrange("p t c -> p c t"))

        def quantise_weights(n, g_from, g_to):
            if g_from == 0:
                w_codes[n] = w_keep.tile([P, K_PASSES * GROUP_F], U32, align_bytes=64, name="w_codes")
                w_scales[n] = w_keep.tile([P, K_PASSES * GROUP_F], U8, align_bytes=64, name="w_scales")
            cols = slice(g_from * GROUP_F, g_to * GROUP_F)
            nc.vector.quantize_mx(
                out=w_codes[n][:, cols].bitcast(FP8X4),
                scales=w_scales[n][:, cols],
                in_=w_grouped[n][:, g_from:g_to, :, :].rearrange("p g c t -> p (g c t)"),
            )

        bias = const.tile([P, P], F32)
        norm_params = const.tile([P, P], F32)
        neg_bias = const.tile([P, n_ft], F32)
        shift3 = const.tile([P, n_ft], F32)
        owed = {m: const.tile([P, n_ft], F32, name="owed%d" % m) for m in set(BY_SCALAR)}

        def spread_rows(rows, table):
            cols = psum_tp.tile([P, P], BF16, tag="tp", name="cols")
            nc.tensor.transpose(cols[:], rows[:], ident_bf16[:])
            nc.scalar.copy(out=table[:], in_=cols[:])

        def spread_biases():
            spread_rows(bias_rows, bias)

        def spread_norm_params():
            spread_rows(norm_rows, norm_params)

        def owed_terms():
            nc.vector.tensor_scalar_mul(out=neg_bias[:], in0=bias[:, 0:n_ft], scalar1=-1.0)
            nc.vector.tensor_scalar_mul(
                out=shift3[:], in0=norm_params[:, n_ft : 2 * n_ft], scalar1=float(LAYERS)
            )
            for m in set(BY_SCALAR):
                nc.vector.scalar_tensor_tensor(
                    out=owed[m][:], in0=bias[:, 0:n_ft], scalar=float(LAYERS - m), in1=shift3[:], op0=ALU.mult, op1=ALU.add
                )

        relus = {}
        ln_term = {}

        def feature_tile(n, i):
            t, half = GROUP_OF[n]
            return t * F_TILES + half * GROUP + i

        def project(n, i, l):
            ft = feature_tile(n, i)
            acc = psum_acc.tile([P, TOK], F32, tag="acc", name="acc")
            for g in range(K_PASSES):
                w_cols = slice(g * GROUP_F + i * P, g * GROUP_F + (i + 1) * P)
                x_cols = slice((l * K_PASSES + g) * TOK, (l * K_PASSES + g + 1) * TOK)
                nc.tensor.matmul_mx(
                    out=acc[:],
                    lhsT=w_codes[n][:, w_cols].bitcast(FP8X4),
                    lhsT_scale=w_scales[n][:, w_cols],
                    rhs=x_codes[:, x_cols].bitcast(FP8X4),
                    rhs_scale=x_scales[:, x_cols],
                    start=(g == 0),
                    stop=(g == K_PASSES - 1),
                )
            if l < BY_SCALAR[n]:
                relu = sums.tile([P, TOK], F32, name="relu")
                nc.scalar.activation(
                    out=relu[:], in_=acc[:], func=ACT.Relu, bias=bias[:, ft : ft + 1], scale=1.0
                )
                relus.setdefault(ft, []).append(relu)
            else:
                total = ln_term[ft]
                nc.vector.scalar_tensor_tensor(
                    out=total[:], in0=acc[:], scalar=neg_bias[:, ft : ft + 1], in1=total[:], op0=ALU.max, op1=ALU.add
                )

        n_rt = LAYERS * TOK_TILES
        chunks = DIM // STATS_MAX
        stats = const.tile([P, n_rt, chunks, STATS], F32)
        mean_var = const.tile([P, n_rt, 2], F32)
        rstd = const.tile([P, n_rt], F32)
        neg_mean = const.tile([P, n_rt], F32)
        z_part = {}

        def tile_statistics(l, j):
            rt = l * TOK_TILES + j
            for c in range(chunks):
                nc.vector.bn_stats(out=stats[:, rt, c, :], in_=x_sb[:, rt, c * STATS_MAX : (c + 1) * STATS_MAX])

        def aggregate(l):
            for j in range(TOK_TILES):
                rt = l * TOK_TILES + j
                nc.vector.bn_aggr(out=mean_var[:, rt, :], in_=stats[:, rt, :, :].rearrange("p c s -> p (c s)"))

        def layer_scales(l):
            rts = slice(l * TOK_TILES, (l + 1) * TOK_TILES)
            nc.scalar.activation(
                out=rstd[:, rts], in_=mean_var[:, rts, 1], func=ACT.Abs_reciprocal_sqrt, bias=eps[:, 0:1], scale=1.0
            )
            if l < LAYERS - 1:
                nc.gpsimd.tensor_scalar(
                    out=neg_mean[:, rts], in0=mean_var[:, rts, 0], scalar1=-1.0, scalar2=0.0, op0=ALU.mult, op1=ALU.add
                )

        def normalised_parts(l, half, engine):
            for j in range(TOK_TILES):
                rt = l * TOK_TILES + j
                z_part[l, j, half] = norm_pool.tile([P, BANK], F32, name="z_part", tag="norm")
                on_vector = engine == "vector"
                (nc.vector if on_vector else nc.gpsimd).tensor_scalar(
                    out=z_part[l, j, half][:],
                    in0=x_sb[:, rt, half * BANK : (half + 1) * BANK],
                    scalar1=mean_var[:, rt, 0:1] if on_vector else neg_mean[:, rt : rt + 1],
                    scalar2=rstd[:, rt : rt + 1],
                    op0=ALU.subtract if on_vector else ALU.add,
                    op1=ALU.mult,
                )

        def norm_terms(f, ts=range(PROJ)):
            half, f_in_half = divmod(f, BANK // P)
            f_cols = slice(f_in_half * P, (f_in_half + 1) * P)
            zt = psum_tp.tile([P, BANK], F32, tag="tp", name="zt")
            for j in range(TOK_TILES):
                for l in range(LAYERS):
                    nc.tensor.matmul(
                        out=zt[:, j * P : (j + 1) * P],
                        lhsT=z_part[l, j, half][:, f_cols],
                        rhs=ident_f32[:],
                        is_transpose=True,
                        start=(l == 0),
                        stop=(l == LAYERS - 1),
                    )
            for t in ts:
                ft = t * F_TILES + f
                n = half * PROJ + t
                ln_term[ft] = norm_pool.tile([P, TOK], F32, name="ln_term", tag="norm")
                nc.scalar.activation(
                    out=ln_term[ft][:], in_=zt[:], func=ACT.Identity,
                    scale=norm_params[:, ft : ft + 1], bias=owed[BY_SCALAR[n]][:, ft : ft + 1],
                )

        def merge_layers(n, i):
            ft = feature_tile(n, i)
            first = relus[ft][0]
            for other in relus[ft][1:]:
                nc.gpsimd.tensor_tensor(out=first[:], in0=first[:], in1=other[:], op=ALU.add)
            relus[ft] = [first]

        def merge(n, i):
            ft = feature_tile(n, i)
            for relu in relus.get(ft, []):
                nc.gpsimd.tensor_tensor(out=ln_term[ft][:], in0=ln_term[ft][:], in1=relu[:], op=ALU.add)

        def turn_back(n, pair, b, engine):
            t, half = GROUP_OF[n]
            back = psum_tp.tile([P, SEQ // P, PAIR_F], F32, tag="tp", name="back")
            for h in range(SEQ // P):
                j = b * (SEQ // P) + h
                for e in range(2):
                    ft = feature_tile(n, 2 * pair + e)
                    nc.tensor.transpose(
                        back[:, h, e * P : (e + 1) * P], ln_term[ft][:, j * P : (j + 1) * P], ident_f32[:]
                    )
            rows = rows_pool.tile([P, SEQ // P, PAIR_F], F32, name="rows")
            if engine == "vector":
                nc.vector.tensor_copy(out=rows[:], in_=back[:])
            else:
                nc.scalar.copy(out=rows[:], in_=back[:])
            f0 = half * GROUP_F + pair * PAIR_F
            nc.sync.dma_start(
                out=outs[t][b, :, f0 : f0 + PAIR_F].rearrange("(p h) f -> p h f", p=P), in_=rows[:]
            )

        def turn_one_back(n, i):
            t, half = GROUP_OF[n]
            ft = feature_tile(n, i)
            f0 = half * GROUP_F + i * P
            for b in range(BATCH):
                back = psum_tp.tile([P, SEQ // P, P], F32, tag="tp", name="back")
                for h in range(SEQ // P):
                    j = b * (SEQ // P) + h
                    nc.tensor.transpose(back[:, h, :], ln_term[ft][:, j * P : (j + 1) * P], ident_f32[:])
                rows = rows_pool.tile([P, SEQ // P, P], F32, name="rows")
                if b == 0:
                    nc.scalar.copy(out=rows[:], in_=back[:])
                else:
                    nc.vector.tensor_copy(out=rows[:], in_=back[:])
                nc.sync.dma_start(
                    out=outs[t][b, :, f0 : f0 + P].rearrange("(p h) f -> p h f", p=P), in_=rows[:]
                )

        def stat_tiles(l, *js):
            for j in js:
                tile_statistics(l, j)

        def turn_layer(l):
            for j in range(TOK_TILES):
                turn_tokens(l, j)
                keep_warm(2)

        def project_group(n, l):
            for i in range(GROUP):
                project(n, i, l)

        def project_pair(n, pair, *between):
            for k in range(2 * LAYERS):
                l, e = divmod(k, 2)
                project(n, 2 * pair + e, l)
                if k % LAYERS == LAYERS - 1 and k // LAYERS < len(between):
                    between[k // LAYERS]()

        def turn_pair_back(n, pair, *engines):
            for b in range(BATCH):
                turn_back(n, pair, b, engines[b])

        def norm_run(f, ts=range(PROJ)):
            return lambda: norm_terms(f, ts)

        def back_run(n, pair, *engines):
            return lambda: turn_pair_back(n, pair, *engines)

        keep_warm(8)
        turn_layer(0)
        stat_tiles(0, 0, 1, 2, 3)
        turn_layer(1)
        aggregate(0)
        layer_scales(0)
        regroup_weights(0, 0, "gpsimd")
        stat_tiles(1, 0, 1, 2, 3)
        quantise_layer(0)
        normalised_parts(0, 0, "gpsimd")
        regroup_weights(0, 1, "scalar")
        aggregate(1)
        layer_scales(1)
        quantise_layer(1)
        turn_layer(2)
        spread_biases()
        stat_tiles(2, 0)
        quantise_weights(0, 0, 2)
        normalised_parts(1, 0, "gpsimd")
        regroup_weights(1, 0, "gpsimd")
        stat_tiles(2, 1)
        keep_warm(3)
        project_group(0, 0)
        spread_norm_params()
        quantise_layer(2)
        stat_tiles(2, 2, 3)
        aggregate(2)
        layer_scales(2)
        project_group(0, 1)
        owed_terms()
        normalised_parts(2, 0, "vector")
        normalised_parts(0, 1, "gpsimd")
        normalised_parts(1, 1, "gpsimd")
        regroup_weights(1, 1, "vector")
        project(0, 0, 2)
        project(0, 1, 2)
        norm_terms(0, (1, 2, 0))
        quantise_weights(1, 0, 2)
        project(0, 2, 2)
        project(0, 3, 2)
        norm_terms(1, (1, 2, 0))
        load_weights(3)
        normalised_parts(2, 1, "vector")
        regroup_weights(2, 0, "vector")
        project_pair(1, 0, norm_run(2, (1, 2, 0)), norm_run(3, (1, 2, 0)))
        load_weights(4)
        regroup_weights(2, 1, "vector")
        quantise_weights(2, 0, 2)
        project_pair(1, 1, norm_run(4), norm_run(5))
        for i in range(GROUP):
            merge_layers(0, i)
        for i in range(GROUP):
            merge(0, i)
        regroup_weights(3, 0, "scalar")
        project_pair(2, 0, norm_run(6), norm_run(7))
        load_weights(5)
        regroup_weights(3, 1, "vector")
        quantise_weights(3, 0, 2)
        project_pair(2, 1, back_run(1, 0, "scalar", "scalar"), back_run(1, 1, "scalar", "scalar"))
        regroup_weights(4, 0, "scalar")
        project_pair(3, 0, back_run(0, 0, "scalar", "scalar"), back_run(0, 1, "scalar", "scalar"))
        regroup_weights(4, 1, "vector")
        quantise_weights(4, 0, 2)
        regroup_weights(5, 0, "scalar")
        project_pair(3, 1, back_run(2, 0, "scalar", "scalar"), back_run(2, 1, "scalar", "scalar"))
        regroup_weights(5, 1, "scalar")
        project_pair(4, 0, back_run(3, 0, "scalar", "scalar"))
        quantise_weights(5, 0, 2)
        project_pair(4, 1, back_run(3, 1, "scalar", "scalar"))
        project_pair(5, 0, back_run(4, 0, "scalar", "scalar"))
        for l in range(LAYERS):
            project(5, 2, l)
        turn_pair_back(4, 1, "scalar", "scalar")
        project(5, 3, 0)
        project(5, 3, 1)
        turn_pair_back(5, 0, "scalar", "scalar")
        turn_one_back(5, 2)
        project(5, 3, 2)
        turn_one_back(5, 3)
